import numpy as np
import ml_dtypes


def mxq(x, axis, fmt="e4m3"):
    dtype, down = {"e4m3": (ml_dtypes.float8_e4m3fn, 7), "e5m2": (ml_dtypes.float8_e5m2, 14)}[fmt]
    v = np.moveaxis(np.asarray(x, np.float32).astype(ml_dtypes.bfloat16).astype(np.float64), axis, -1)
    blocks = v.reshape(v.shape[:-1] + (-1, 32))
    amax = np.abs(blocks).max(-1, keepdims=True)
    byte = np.maximum(np.where(amax > 0, np.frexp(amax)[1] - 1 + 127, 0) - down, 1)
    scale = np.exp2(byte - 127.0)
    codes = (blocks / scale).astype(np.float32).astype(dtype).astype(np.float64)
    return np.moveaxis((codes * scale).reshape(v.shape), -1, axis)


WIDE = False


def mx_kscale(k):
    if not WIDE:
        return np.ones(k)
    levels = np.array([10, -10, 5, -5, 0])
    a = np.random.permutation(np.resize(levels, k // 512 * 4)).reshape(k // 512, 4)
    idx = np.arange(k)
    return np.exp2(a[idx // 512, idx % 128 // 32])


BF16 = ml_dtypes.bfloat16


def bf(x):
    return np.asarray(x, np.float32).astype(BF16)


def f64(x):
    return np.asarray(x).astype(np.float64)


E2M1 = np.array([0.0, 0.5, 1.0, 1.5, 2.0, 3.0, 4.0, 6.0, -0.0, -0.5, -1.0, -1.5, -2.0, -3.0, -4.0, -6.0])


def pack_weight(w, fmt):
    k, n = w.shape
    w = f64(bf(w)).reshape(k // 32, 32, n)
    amax = np.abs(w).max(1)
    if fmt == "e4m3":
        byte = np.frexp(amax)[1] - 1 + 127 - 7
    else:
        mant, ex = np.frexp(amax / 6.0)
        byte = np.where(mant > 0.5, ex, ex - 1) + 127
    byte = np.clip(np.where(amax > 0, byte, 1), 1, 254)
    scaled = (w * np.exp2(127.0 - byte)[:, None, :]).reshape(k, n).astype(np.float32)
    by_word = np.ascontiguousarray(scaled.reshape(k // 512, 128, 4, n).transpose(0, 1, 3, 2))
    if fmt == "e4m3":
        words = by_word.astype(ml_dtypes.float8_e4m3fn).view(np.uint8)
    else:
        c = by_word.astype(ml_dtypes.float4_e2m1fn).view(np.uint8) & 0xF
        words = c[..., 0::2] | (c[..., 1::2] << 4)
    return np.ascontiguousarray(words), np.ascontiguousarray(byte.astype(np.uint8).reshape(k // 512, 16, n))


def unpack_weight(words, scales, fmt):
    g, p, n, _ = words.shape
    if fmt == "e4m3":
        vals = np.ascontiguousarray(words).view(ml_dtypes.float8_e4m3fn).astype(np.float64)
    else:
        nib = np.empty((g, p, n, 4), np.uint8)
        nib[..., 0::2] = words & 0xF
        nib[..., 1::2] = words >> 4
        vals = E2M1[nib]
    vals = vals * np.repeat(np.exp2(scales.astype(np.float64) - 127.0), 8, axis=1)[..., None]
    return vals.transpose(0, 1, 3, 2).reshape(g * 512, n)


B, L, D, E, S, H = 4, 2048, 512, 16, 32, 512
K = E * S


def softmax(v):
    e = np.exp(v - v.max(-1, keepdims=True))
    return e / e.sum(-1, keepdims=True)


def setup_inputs():
    s = mx_kscale(H)
    h = bf(np.random.standard_normal((B, E, S, H)) * 0.6 * s)
    w2 = np.random.standard_normal((E, H, D)) * 1.5 / np.sqrt(H) / s[:, None]
    w2_words, w2_scales = pack_weight(w2.reshape(-1, D), "e4m3")
    b2 = bf(np.random.standard_normal((E, D)) * 0.5)
    logits = bf(np.random.standard_normal((B, L, E, S)) * 2.0)
    return {"h": h,
            "w2_words": w2_words,
            "w2_scales": w2_scales,
            "b2": b2,
            "logits": logits}


def reference(h, w2_words, w2_scales, b2, logits):
    eo = (mxq(f64(h), 3, "e4m3") @ unpack_weight(w2_words, w2_scales, "e4m3").reshape(E, H, D)) + f64(b2)[:, None, :]
    eo = eo.reshape(B, K, D)
    c_w = softmax(f64(logits).reshape(B, L, K))
    return mxq(c_w, 2, "e4m3") @ mxq(eo, 1, "e4m3")

@@ -1,0 +1,286 @@
+from concourse import mybir
+from concourse.masks import make_identity
+
+F32 = mybir.dt.float32
+BF16 = mybir.dt.bfloat16
+I32 = mybir.dt.int32
+U32 = mybir.dt.uint32
+U8 = mybir.dt.uint8
+FP8X4 = mybir.dt.float8_e4m3fn_x4
+ALU = mybir.AluOpType
+ACT = mybir.ActivationFunctionType
+
+P = 128
+B, L, D, E, S, H = 4, 2048, 512, 16, 32, 512
+K = E * S
+J = 4
+GROUPS = B * L // (P * J)
+GROUPS_PER_BATCH = GROUPS // B
+D_CHUNKS = D // P
+FOLDS = 3
+X_BUFS = 6
+
+FLOPS = 2 * B * E * S * H * D + 2 * B * L * K * D
+
+
+def tile_softmoe_pb_t_e_kernel(tc, h, w2_words, w2_scales, b2, logits, out):
+    nc = tc.nc
+
+    logits_rows = logits.rearrange("b l e s -> (b l) (e s)")
+    out_rows = out.rearrange("b l d -> (b l) d")
+
+    with tc.manual_schedule(), \
+            tc.tile_pool(name="const", bufs=1) as const, \
+            tc.tile_pool(name="small", bufs=3) as small, \
+            tc.tile_pool(name="xs", bufs=X_BUFS) as xs, \
+            tc.tile_pool(name="work", bufs=2) as work, \
+            tc.tile_pool(name="cwq", bufs=4) as cwq, \
+            tc.psum_pool(name="psum_t", bufs=4) as psum_t, \
+            tc.psum_pool(name="psum_mm", bufs=4) as psum_mm:
+
+        ident_f32 = const.tile([P, P], F32)
+        make_identity(nc, ident_f32[:])
+        ident_bf16 = const.tile([P, P], BF16)
+        nc.vector.tensor_copy(out=ident_bf16[:], in_=ident_f32[:])
+        warm = const.tile([P, 1], F32)
+        nc.vector.memset(warm[:], 0.0)
+        nc.scalar.activation(out=warm[:], in_=warm[:], func=ACT.Exp)
+
+        eo_codes = const.tile([P, B, D], U32, align_bytes=64)
+        eo_scales = const.tile([P, B, D], U8, align_bytes=64)
+
+        x_of, folded, neg_max_of, ex_of, ex_sum_of, inv_sum_of = {}, {}, {}, {}, {}, {}
+        cw_of, banks_of, cw_t_of, codes_of, scales_of = {}, {}, {}, {}, {}
+
+        def is_group(g):
+            return 0 <= g < GROUPS
+
+        def load(g):
+            if not is_group(g):
+                return
+            rows = logits_rows[g * P * J:(g + 1) * P * J, :]
+            x = xs.tile([P, J, K], BF16)
+            nc.sync.dma_start(out=x[:], in_=rows.rearrange("(p j) k -> p j k", j=J))
+            x_of[g] = x
+
+        def fold_max(g, level):
+            if not is_group(g):
+                return
+            wide = x_of[g] if level == 0 else folded[(g, level - 1)]
+            width = K >> (level + 1)
+            half = work.tile([P, J, width], BF16, name="fold%d" % level)
+            nc.vector.tensor_tensor(out=half[:], in0=wide[:, :, 0:width], in1=wide[:, :, width:2 * width],
+                                    op=ALU.max)
+            folded[(g, level)] = half
+
+        def finish_max(g):
+            if not is_group(g):
+                return
+            neg_max = small.tile([P, J], F32)
+            nc.vector.tensor_reduce(out=neg_max[:], in_=folded[(g, FOLDS - 1)][:],
+                                    axis=mybir.AxisListType.X, op=ALU.max, negate=True)
+            neg_max_of[g] = neg_max
+
+        def exps(g):
+            if not is_group(g):
+                return
+            ex = work.tile([P, J, K], F32)
+            ex_sum = small.tile([P, J], F32)
+            for j in range(J):
+                nc.scalar.activation(out=ex[:, j, :], in_=x_of[g][:, j, :], func=ACT.Exp,
+                                     bias=neg_max_of[g][:, j:j + 1], scale=1.0,
+                                     accum_out=ex_sum[:, j:j + 1])
+            ex_of[g], ex_sum_of[g] = ex, ex_sum
+
+        def invert_sum(g):
+            if not is_group(g):
+                return
+            inv_sum = small.tile([P, J], F32)
+            nc.vector.reciprocal(out=inv_sum[:], in_=ex_sum_of[g][:])
+            inv_sum_of[g] = inv_sum
+            cw = work.tile([P, J, K], BF16)
+            cw_of[g] = cw
+
+        def normalise(g, j):
+            if not is_group(g):
+                return
+            nc.vector.tensor_scalar(out=cw_of[g][:, j, :], in0=ex_of[g][:, j, :],
+                                    scalar1=inv_sum_of[g][:, j:j + 1], scalar2=None, op0=ALU.mult)
+
+        def transposes(g):
+            if not is_group(g):
+                return
+            for pair in range(J // 2):
+                bank = psum_t.tile([P, 2, 2, P], F32, tag="bank_t")
+                for i in range(2):
+                    words = cw_of[g][:, 2 * pair + i, :].bitcast(F32)
+                    for u in range(2):
+                        nc.tensor.transpose(bank[:, u, i, :], words[:, u * P:(u + 1) * P], ident_f32[:])
+                banks_of[(g, pair)] = bank
+
+        def copy_out(g, pair):
+            if not is_group(g):
+                return
+            if pair == 0:
+                cw_t = work.tile([P, J, P, 4], BF16, align_bytes=64)
+                cw_t_of[g] = cw_t
+            nc.vector.tensor_copy(out=cw_t_of[g][:].bitcast(F32)[:, 2 * pair:2 * pair + 2, :, :],
+                                  in_=banks_of[(g, pair)][:].rearrange("q u i l -> q i l u"))
+
+        def quantise(g):
+            if not is_group(g):
+                return
+            codes = cwq.tile([P, J * P], U32, align_bytes=64)
+            scales = cwq.tile([P, J * P], U8, align_bytes=64)
+            nc.vector.quantize_mx(out=codes[:].bitcast(FP8X4), scales=scales[:],
+                                  in_=cw_t_of[g][:].rearrange("q j l t -> q (j l t)"))
+            codes_of[g], scales_of[g] = codes, scales
+
+        def combine(g, outs, shared):
+            if not is_group(g):
+                return
+            b = g // GROUPS_PER_BATCH
+            o = outs.tile([P, J, D], F32)
+            for j in range(J):
+                acc = psum_mm.tile([P, D], F32, tag="bank_mm")
+                nc.tensor.matmul_mx(out=acc[:],
+                                    lhsT=codes_of[g][:, j * P:(j + 1) * P].bitcast(FP8X4),
+                                    lhsT_scale=scales_of[g][:, j * P:(j + 1) * P],
+                                    rhs=eo_codes[:, b, :].bitcast(FP8X4),
+                                    rhs_scale=eo_scales[:, b, :],
+                                    start=True, stop=True)
+                if shared and j % 2 == 1:
+                    nc.vector.tensor_copy(out=o[:, j, :], in_=acc[:])
+                else:
+                    nc.scalar.copy(out=o[:, j, :], in_=acc[:])
+            rows = out_rows[g * P * J:(g + 1) * P * J, :]
+            nc.scalar.dma_start(out=rows.rearrange("(p j) d -> p j d", j=J), in_=o[:])
+
+        def step(i, outs):
+            load(i + X_BUFS - 1)
+            fold_max(i + 1, 0)
+            copy_out(i - 1, 0)
+            fold_max(i + 1, 1)
+            copy_out(i - 1, 1)
+            fold_max(i + 1, 2)
+            invert_sum(i)
+            finish_max(i + 1)
+            exps(i + 1)
+            normalise(i, 0)
+            normalise(i, 1)
+            quantise(i - 1)
+            normalise(i, 2)
+            normalise(i, 3)
+            if outs is not None:
+                combine(i - 1, outs, i - 1 == GROUPS - 1)
+            transposes(i)
+
+        with tc.tile_pool(name="experts", bufs=1) as experts:
+            w2_planes = experts.tile([P, E, D], U8, align_bytes=64)
+            nc.vector.memset(w2_planes[:].bitcast(I32), 0)
+            b2_rows = experts.tile([P, D], BF16)
+            nc.vector.memset(b2_rows[:], 0.0)
+
+            for g in range(3):
+                load(g)
+            h_rows = experts.tile([P, B * E * S // P, H], BF16)
+            nc.sync.dma_start(out=h_rows[:],
+                              in_=h.rearrange("b e s k -> (b e s) k").rearrange("(n p) k -> p n k", p=P))
+            scale_rows = w2_scales.rearrange("g (qq r) n -> r qq g n", r=4)
+            for r in range(4):
+                nc.sync.dma_start(out=w2_planes[r:P:32, :, :].bitcast(I32),
+                                  in_=scale_rows[r].bitcast(I32))
+            nc.sync.dma_start(out=b2_rows[0:E, :], in_=b2)
+            load(3)
+            w2_codes = experts.tile([P, E, D], U32, align_bytes=64)
+            w2_words_by_p = w2_words.rearrange("g p n t -> p g (n t)").bitcast(I32)
+            for e0 in range(0, E, 4):
+                nc.sync.dma_start(out=w2_codes[:, e0:e0 + 4, :].bitcast(I32),
+                                  in_=w2_words_by_p[:, e0:e0 + 4, :])
+
+            h_t = experts.tile([P, E, B, S, 4], BF16, align_bytes=64)
+            h_codes = experts.tile([P, E, B * S], U32, align_bytes=64)
+            h_scales = experts.tile([P, E, B * S], U8, align_bytes=64)
+            b2_t = experts.tile([P, D_CHUNKS, E], F32)
+            eo_t = experts.tile([P, D_CHUNKS, B, E, S], BF16)
+            eo_k = experts.tile([P, B, D, 4], BF16, align_bytes=64)
+
+            def h_to_partitions():
+                b2_bank = psum_mm.tile([P, D_CHUNKS, P], BF16, tag="bank_mm")
+                for c in range(D_CHUNKS):
+                    nc.tensor.transpose(b2_bank[:, c, :], b2_rows[:, c * P:(c + 1) * P], ident_bf16[:])
+                nc.scalar.copy(out=b2_t[:], in_=b2_bank[:, :, 0:E])
+                h_t_words = h_t[:].bitcast(F32)
+                for half in range(2):
+                    for b in range(B):
+                        bank = psum_mm.tile([P, 2, 2, P], F32, tag="bank_mm")
+                        for i in range(2):
+                            words = h_rows[:, 4 * b + 2 * half + i, :].bitcast(F32)
+                            for u in range(2):
+                                nc.tensor.transpose(bank[:, u, i, :], words[:, u:H // 2:2], ident_f32[:])
+                        nc.scalar.copy(out=h_t_words[:, 8 * half:8 * half + 8, b, :, :],
+                                       in_=bank[:].rearrange("p u i (q s) -> p (i q) s u", s=S))
+
+            def quantise_h():
+                for half in range(2):
+                    some = slice(8 * half, 8 * half + 8)
+                    nc.vector.quantize_mx(
+                        out=h_codes[:, some, :].rearrange("p e m -> p (e m)").bitcast(FP8X4),
+                        scales=h_scales[:, some, :].rearrange("p e m -> p (e m)"),
+                        in_=h_t[:, some, :, :, :].rearrange("p e b s t -> p (e b s t)"))
+
+            def expert_layer():
+                for e in range(E):
+                    acc = psum_mm.tile([P, D_CHUNKS, B * S], F32, tag="bank_mm")
+                    for c in range(D_CHUNKS):
+                        nc.tensor.matmul_mx(out=acc[:, c, :],
+                                            lhsT=w2_codes[:, e, c * P:(c + 1) * P].bitcast(FP8X4),
+                                            lhsT_scale=w2_planes[:, e, c * P:(c + 1) * P],
+                                            rhs=h_codes[:, e, :].bitcast(FP8X4),
+                                            rhs_scale=h_scales[:, e, :],
+                                            start=True, stop=True)
+                    if e % 2 == 0:
+                        nc.vector.tensor_tensor(
+                            out=eo_t[:, :, :, e, :],
+                            in0=acc[:].rearrange("p c (b s) -> p c b s", s=S),
+                            in1=b2_t[:, :, e:e + 1].unsqueeze(3).to_broadcast([P, D_CHUNKS, B, S]),
+                            op=ALU.add)
+                    else:
+                        for c in range(D_CHUNKS):
+                            nc.scalar.activation(out=eo_t[:, c, :, e, :],
+                                                 in_=acc[:, c, :].rearrange("p (b s) -> p b s", s=S),
+                                                 func=ACT.Identity, bias=b2_t[:, c, e:e + 1], scale=1.0)
+
+            def eo_to_partitions():
+                eo_k_words = eo_k[:].bitcast(F32)
+                for b in range(B):
+                    for half in range(2):
+                        bank = psum_mm.tile([P, 2, 2 * P], F32, tag="bank_mm")
+                        for i in range(2):
+                            words = eo_t[:, 2 * half + i, b, :, :].rearrange("p e s -> p (e s)").bitcast(F32)
+                            for u in range(2):
+                                nc.tensor.transpose(bank[:, u, i * P:(i + 1) * P],
+                                                    words[:, u * P:(u + 1) * P], ident_f32[:])
+                        nc.scalar.copy(out=eo_k_words[:, b, 2 * half * P:2 * (half + 1) * P, :],
+                                       in_=bank[:].rearrange("q u d -> q d u"))
+
+            def quantise_eo():
+                for b in range(B):
+                    nc.vector.quantize_mx(out=eo_codes[:, b, :].bitcast(FP8X4), scales=eo_scales[:, b, :],
+                                          in_=eo_k[:, b, :, :].rearrange("q d t -> q (d t)"))
+
+            step(-1, None)
+            step(0, None)
+            h_to_partitions()
+            step(1, None)
+            quantise_h()
+            expert_layer()
+            eo_to_partitions()
+            step(2, None)
+            quantise_eo()
+
+        with tc.tile_pool(name="outs", bufs=3) as outs:
+            combine(0, outs, True)
+            combine(1, outs, True)
+            for i in range(3, GROUPS + 1):
+                step(i, outs)

@@ -18,7 +18,14 @@ GROUPS = B * L // (P * J)
 GROUPS_PER_BATCH = GROUPS // B
 D_CHUNKS = D // P
 FOLDS = 3
-X_BUFS = 6
+LOAD_AHEAD = 4
+
+FIRST_STEP = -2
+H_STEP = 1
+W_STEP = H_STEP + 2
+EO_STEP = W_STEP + 4
+OUT_STEP = EO_STEP + 2
+LAST_STEP = GROUPS + 1
 
 FLOPS = 2 * B * E * S * H * D + 2 * B * L * K * D
 
@@ -31,10 +38,11 @@ def tile_softmoe_pb_t_e_kernel(tc, h, w2_words, w2_scales, b2, logits, out):
 
     with tc.manual_schedule(), \
             tc.tile_pool(name="const", bufs=1) as const, \
-            tc.tile_pool(name="small", bufs=3) as small, \
-            tc.tile_pool(name="xs", bufs=X_BUFS) as xs, \
-            tc.tile_pool(name="work", bufs=2) as work, \
-            tc.tile_pool(name="cwq", bufs=4) as cwq, \
+            tc.tile_pool(name="small", bufs=4) as small, \
+            tc.tile_pool(name="xs", bufs=6) as xs, \
+            tc.tile_pool(name="work", bufs=3) as work, \
+            tc.tile_pool(name="stage", bufs=2) as stage, \
+            tc.tile_pool(name="cwq", bufs=10) as cwq, \
             tc.psum_pool(name="psum_t", bufs=4) as psum_t, \
             tc.psum_pool(name="psum_mm", bufs=4) as psum_mm:
 
@@ -56,7 +64,7 @@ def tile_softmoe_pb_t_e_kernel(tc, h, w2_words, w2_scales, b2, logits, out):
             return 0 <= g < GROUPS
 
         def load(g):
-            if not is_group(g):
+            if not is_group(g) or g in x_of:
                 return
             rows = logits_rows[g * P * J:(g + 1) * P * J, :]
             x = xs.tile([P, J, K], BF16)
@@ -68,7 +76,7 @@ def tile_softmoe_pb_t_e_kernel(tc, h, w2_words, w2_scales, b2, logits, out):
                 return
             wide = x_of[g] if level == 0 else folded[(g, level - 1)]
             width = K >> (level + 1)
-            half = work.tile([P, J, width], BF16, name="fold%d" % level)
+            half = stage.tile([P, J, width], BF16, name="fold%d" % level)
             nc.vector.tensor_tensor(out=half[:], in0=wide[:, :, 0:width], in1=wide[:, :, width:2 * width],
                                     op=ALU.max)
             folded[(g, level)] = half
@@ -98,14 +106,16 @@ def tile_softmoe_pb_t_e_kernel(tc, h, w2_words, w2_scales, b2, logits, out):
             inv_sum = small.tile([P, J], F32)
             nc.vector.reciprocal(out=inv_sum[:], in_=ex_sum_of[g][:])
             inv_sum_of[g] = inv_sum
-            cw = work.tile([P, J, K], BF16)
-            cw_of[g] = cw
 
-        def normalise(g, j):
+        def normalise(g):
             if not is_group(g):
                 return
-            nc.vector.tensor_scalar(out=cw_of[g][:, j, :], in0=ex_of[g][:, j, :],
-                                    scalar1=inv_sum_of[g][:, j:j + 1], scalar2=None, op0=ALU.mult)
+            cw = work.tile([P, J, K], BF16)
+            for j in range(J):
+                nc.gpsimd.tensor_scalar(out=cw[:, j, :], in0=ex_of[g][:, j, :],
+                                        scalar1=inv_sum_of[g][:, j:j + 1], scalar2=0.0,
+                                        op0=ALU.mult, op1=ALU.add)
+            cw_of[g] = cw
 
         def transposes(g):
             if not is_group(g):
@@ -118,14 +128,18 @@ def tile_softmoe_pb_t_e_kernel(tc, h, w2_words, w2_scales, b2, logits, out):
                         nc.tensor.transpose(bank[:, u, i, :], words[:, u * P:(u + 1) * P], ident_f32[:])
                 banks_of[(g, pair)] = bank
 
-        def copy_out(g, pair):
+        def copy_out(g, pair, on_scalar):
             if not is_group(g):
                 return
             if pair == 0:
-                cw_t = work.tile([P, J, P, 4], BF16, align_bytes=64)
+                cw_t = stage.tile([P, J, P, 4], BF16, align_bytes=64)
                 cw_t_of[g] = cw_t
-            nc.vector.tensor_copy(out=cw_t_of[g][:].bitcast(F32)[:, 2 * pair:2 * pair + 2, :, :],
-                                  in_=banks_of[(g, pair)][:].rearrange("q u i l -> q i l u"))
+            words = cw_t_of[g][:].bitcast(F32)[:, 2 * pair:2 * pair + 2, :, :]
+            bank = banks_of[(g, pair)][:].rearrange("q u i l -> q i l u")
+            if on_scalar:
+                nc.scalar.copy(out=words, in_=bank)
+            else:
+                nc.vector.tensor_copy(out=words, in_=bank)
 
         def quantise(g):
             if not is_group(g):
@@ -136,9 +150,21 @@ def tile_softmoe_pb_t_e_kernel(tc, h, w2_words, w2_scales, b2, logits, out):
                                   in_=cw_t_of[g][:].rearrange("q j l t -> q (j l t)"))
             codes_of[g], scales_of[g] = codes, scales
 
-        def combine(g, outs, shared):
-            if not is_group(g):
-                return
+        def front(s, copies_on_scalar):
+            load(s + LOAD_AHEAD)
+            transposes(s - 1)
+            fold_max(s + 2, 0)
+            quantise(s - 2)
+            fold_max(s + 2, 1)
+            invert_sum(s)
+            normalise(s)
+            fold_max(s + 2, 2)
+            copy_out(s - 1, 0, copies_on_scalar)
+            finish_max(s + 2)
+            copy_out(s - 1, 1, copies_on_scalar)
+            exps(s + 1)
+
+        def combine(g, outs):
             b = g // GROUPS_PER_BATCH
             o = outs.tile([P, J, D], F32)
             for j in range(J):
@@ -149,138 +175,112 @@ def tile_softmoe_pb_t_e_kernel(tc, h, w2_words, w2_scales, b2, logits, out):
                                     rhs=eo_codes[:, b, :].bitcast(FP8X4),
                                     rhs_scale=eo_scales[:, b, :],
                                     start=True, stop=True)
-                if shared and j % 2 == 1:
-                    nc.vector.tensor_copy(out=o[:, j, :], in_=acc[:])
-                else:
+                if j % 2 == 0:
                     nc.scalar.copy(out=o[:, j, :], in_=acc[:])
+                else:
+                    nc.vector.tensor_copy(out=o[:, j, :], in_=acc[:])
             rows = out_rows[g * P * J:(g + 1) * P * J, :]
             nc.scalar.dma_start(out=rows.rearrange("(p j) d -> p j d", j=J), in_=o[:])
 
-        def step(i, outs):
-            load(i + X_BUFS - 1)
-            fold_max(i + 1, 0)
-            copy_out(i - 1, 0)
-            fold_max(i + 1, 1)
-            copy_out(i - 1, 1)
-            fold_max(i + 1, 2)
-            invert_sum(i)
-            finish_max(i + 1)
-            exps(i + 1)
-            normalise(i, 0)
-            normalise(i, 1)
-            quantise(i - 1)
-            normalise(i, 2)
-            normalise(i, 3)
-            if outs is not None:
-                combine(i - 1, outs, i - 1 == GROUPS - 1)
-            transposes(i)
-
         with tc.tile_pool(name="experts", bufs=1) as experts:
             w2_planes = experts.tile([P, E, D], U8, align_bytes=64)
-            nc.vector.memset(w2_planes[:].bitcast(I32), 0)
-            b2_rows = experts.tile([P, D], BF16)
-            nc.vector.memset(b2_rows[:], 0.0)
-
-            for g in range(3):
-                load(g)
-            h_rows = experts.tile([P, B * E * S // P, H], BF16)
-            nc.sync.dma_start(out=h_rows[:],
-                              in_=h.rearrange("b e s k -> (b e s) k").rearrange("(n p) k -> p n k", p=P))
-            scale_rows = w2_scales.rearrange("g (qq r) n -> r qq g n", r=4)
-            for r in range(4):
-                nc.sync.dma_start(out=w2_planes[r:P:32, :, :].bitcast(I32),
-                                  in_=scale_rows[r].bitcast(I32))
-            nc.sync.dma_start(out=b2_rows[0:E, :], in_=b2)
-            load(3)
             w2_codes = experts.tile([P, E, D], U32, align_bytes=64)
-            w2_words_by_p = w2_words.rearrange("g p n t -> p g (n t)").bitcast(I32)
-            for e0 in range(0, E, 4):
-                nc.sync.dma_start(out=w2_codes[:, e0:e0 + 4, :].bitcast(I32),
-                                  in_=w2_words_by_p[:, e0:e0 + 4, :])
-
-            h_t = experts.tile([P, E, B, S, 4], BF16, align_bytes=64)
             h_codes = experts.tile([P, E, B * S], U32, align_bytes=64)
             h_scales = experts.tile([P, E, B * S], U8, align_bytes=64)
+            b2_rows = experts.tile([P, D], BF16)
             b2_t = experts.tile([P, D_CHUNKS, E], F32)
-            eo_t = experts.tile([P, D_CHUNKS, B, E, S], BF16)
-            eo_k = experts.tile([P, B, D, 4], BF16, align_bytes=64)
+            nc.vector.memset(w2_planes[:].bitcast(I32), 0)
+            nc.vector.memset(b2_rows[:], 0.0)
 
-            def h_to_partitions():
+            with tc.tile_pool(name="h_stage", bufs=1) as h_stage:
+                h_rows = h_stage.tile([P, B * E * S // P, H], BF16)
+                h_t = h_stage.tile([P, E, B, S, 4], BF16, align_bytes=64)
+
+                for g in range(3):
+                    load(g)
+                nc.sync.dma_start(out=h_rows[:],
+                                  in_=h.rearrange("b e s k -> (b e s) k").rearrange("(n p) k -> p n k", p=P))
+                scale_rows = w2_scales.rearrange("g (qq r) n -> r qq g n", r=4)
+                for r in range(4):
+                    nc.sync.dma_start(out=w2_planes[r:P:32, :, :].bitcast(I32),
+                                      in_=scale_rows[r].bitcast(I32))
+                nc.sync.dma_start(out=b2_rows[0:E, :], in_=b2)
+                w2_words_by_p = w2_words.rearrange("g p n t -> p g (n t)").bitcast(I32)
+                for half in range(2):
+                    load(3 + half)
+                    for e0 in (8 * half, 8 * half + 4):
+                        nc.sync.dma_start(out=w2_codes[:, e0:e0 + 4, :].bitcast(I32),
+                                          in_=w2_words_by_p[:, e0:e0 + 4, :])
+
+                for s in range(FIRST_STEP, H_STEP):
+                    front(s, False)
+
                 b2_bank = psum_mm.tile([P, D_CHUNKS, P], BF16, tag="bank_mm")
                 for c in range(D_CHUNKS):
                     nc.tensor.transpose(b2_bank[:, c, :], b2_rows[:, c * P:(c + 1) * P], ident_bf16[:])
                 nc.scalar.copy(out=b2_t[:], in_=b2_bank[:, :, 0:E])
+
                 h_t_words = h_t[:].bitcast(F32)
                 for half in range(2):
+                    front(H_STEP + half, False)
+                    some = slice(8 * half, 8 * half + 8)
                     for b in range(B):
                         bank = psum_mm.tile([P, 2, 2, P], F32, tag="bank_mm")
                         for i in range(2):
                             words = h_rows[:, 4 * b + 2 * half + i, :].bitcast(F32)
                             for u in range(2):
                                 nc.tensor.transpose(bank[:, u, i, :], words[:, u:H // 2:2], ident_f32[:])
-                        nc.scalar.copy(out=h_t_words[:, 8 * half:8 * half + 8, b, :, :],
+                        nc.scalar.copy(out=h_t_words[:, some, b, :, :],
                                        in_=bank[:].rearrange("p u i (q s) -> p (i q) s u", s=S))
-
-            def quantise_h():
-                for half in range(2):
-                    some = slice(8 * half, 8 * half + 8)
                     nc.vector.quantize_mx(
                         out=h_codes[:, some, :].rearrange("p e m -> p (e m)").bitcast(FP8X4),
                         scales=h_scales[:, some, :].rearrange("p e m -> p (e m)"),
                         in_=h_t[:, some, :, :, :].rearrange("p e b s t -> p (e b s t)"))
 
-            def expert_layer():
-                for e in range(E):
-                    acc = psum_mm.tile([P, D_CHUNKS, B * S], F32, tag="bank_mm")
-                    for c in range(D_CHUNKS):
-                        nc.tensor.matmul_mx(out=acc[:, c, :],
-                                            lhsT=w2_codes[:, e, c * P:(c + 1) * P].bitcast(FP8X4),
-                                            lhsT_scale=w2_planes[:, e, c * P:(c + 1) * P],
-                                            rhs=h_codes[:, e, :].bitcast(FP8X4),
-                                            rhs_scale=h_scales[:, e, :],
-                                            start=True, stop=True)
-                    if e % 2 == 0:
+            with tc.tile_pool(name="eo_stage", bufs=1) as eo_stage:
+                eo_t = eo_stage.tile([P, D_CHUNKS, B, E, S], BF16)
+                eo_k = eo_stage.tile([P, B, D, 4], BF16, align_bytes=64)
+
+                for quarter in range(4):
+                    front(W_STEP + quarter, True)
+                    for e in range(4 * quarter, 4 * quarter + 4):
+                        acc = psum_mm.tile([P, D_CHUNKS, B * S], F32, tag="bank_mm")
+                        for c in range(D_CHUNKS):
+                            nc.tensor.matmul_mx(out=acc[:, c, :],
+                                                lhsT=w2_codes[:, e, c * P:(c + 1) * P].bitcast(FP8X4),
+                                                lhsT_scale=w2_planes[:, e, c * P:(c + 1) * P],
+                                                rhs=h_codes[:, e, :].bitcast(FP8X4),
+                                                rhs_scale=h_scales[:, e, :],
+                                                start=True, stop=True)
                         nc.vector.tensor_tensor(
                             out=eo_t[:, :, :, e, :],
                             in0=acc[:].rearrange("p c (b s) -> p c b s", s=S),
                             in1=b2_t[:, :, e:e + 1].unsqueeze(3).to_broadcast([P, D_CHUNKS, B, S]),
                             op=ALU.add)
-                    else:
-                        for c in range(D_CHUNKS):
-                            nc.scalar.activation(out=eo_t[:, c, :, e, :],
-                                                 in_=acc[:, c, :].rearrange("p (b s) -> p b s", s=S),
-                                                 func=ACT.Identity, bias=b2_t[:, c, e:e + 1], scale=1.0)
 
-            def eo_to_partitions():
                 eo_k_words = eo_k[:].bitcast(F32)
-                for b in range(B):
-                    for half in range(2):
-                        bank = psum_mm.tile([P, 2, 2 * P], F32, tag="bank_mm")
-                        for i in range(2):
-                            words = eo_t[:, 2 * half + i, b, :, :].rearrange("p e s -> p (e s)").bitcast(F32)
-                            for u in range(2):
-                                nc.tensor.transpose(bank[:, u, i * P:(i + 1) * P],
-                                                    words[:, u * P:(u + 1) * P], ident_f32[:])
-                        nc.scalar.copy(out=eo_k_words[:, b, 2 * half * P:2 * (half + 1) * P, :],
-                                       in_=bank[:].rearrange("q u d -> q d u"))
+                for pair in range(2):
+                    front(EO_STEP + pair, False)
+                    for b in (2 * pair, 2 * pair + 1):
+                        for half in range(2):
+                            bank = psum_mm.tile([P, 2, 2 * P], F32, tag="bank_mm")
+                            for i in range(2):
+                                words = eo_t[:, 2 * half + i, b, :, :].rearrange("p e s -> p (e s)").bitcast(F32)
+                                for u in range(2):
+                                    nc.tensor.transpose(bank[:, u, i * P:(i + 1) * P],
+                                                        words[:, u * P:(u + 1) * P], ident_f32[:])
+                            nc.scalar.copy(out=eo_k_words[:, b, 2 * half * P:2 * (half + 1) * P, :],
+                                           in_=bank[:].rearrange("q u d -> q d u"))
+                    for b in (2 * pair, 2 * pair + 1):
+                        nc.vector.quantize_mx(out=eo_codes[:, b, :].bitcast(FP8X4),
+                                              scales=eo_scales[:, b, :],
+                                              in_=eo_k[:, b, :, :].rearrange("q d t -> q (d t)"))
 
-            def quantise_eo():
-                for b in range(B):
-                    nc.vector.quantize_mx(out=eo_codes[:, b, :].bitcast(FP8X4), scales=eo_scales[:, b, :],
-                                          in_=eo_k[:, b, :, :].rearrange("q d t -> q (d t)"))
-
-            step(-1, None)
-            step(0, None)
-            h_to_partitions()
-            step(1, None)
-            quantise_h()
-            expert_layer()
-            eo_to_partitions()
-            step(2, None)
-            quantise_eo()
-
-        with tc.tile_pool(name="outs", bufs=3) as outs:
-            combine(0, outs, True)
-            combine(1, outs, True)
-            for i in range(3, GROUPS + 1):
-                step(i, outs)
+        with tc.tile_pool(name="outs", bufs=4) as outs:
+            combined = 0
+            for s in range(OUT_STEP, LAST_STEP + 1):
+                front(s, False)
+                for n in range(2):
+                    if combined <= s - 2:
+                        combine(combined, outs)
+                        combined += 1

@@ -175,10 +175,7 @@ def tile_softmoe_pb_t_e_kernel(tc, h, w2_words, w2_scales, b2, logits, out):
                                     rhs=eo_codes[:, b, :].bitcast(FP8X4),
                                     rhs_scale=eo_scales[:, b, :],
                                     start=True, stop=True)
-                if j % 2 == 0:
-                    nc.scalar.copy(out=o[:, j, :], in_=acc[:])
-                else:
-                    nc.vector.tensor_copy(out=o[:, j, :], in_=acc[:])
+                nc.scalar.copy(out=o[:, j, :], in_=acc[:])
             rows = out_rows[g * P * J:(g + 1) * P * J, :]
             nc.scalar.dma_start(out=rows.rearrange("(p j) d -> p j d", j=J), in_=o[:])
 

@@ -128,18 +128,14 @@ def tile_softmoe_pb_t_e_kernel(tc, h, w2_words, w2_scales, b2, logits, out):
                         nc.tensor.transpose(bank[:, u, i, :], words[:, u * P:(u + 1) * P], ident_f32[:])
                 banks_of[(g, pair)] = bank
 
-        def copy_out(g, pair, on_scalar):
+        def copy_out(g, pair):
             if not is_group(g):
                 return
             if pair == 0:
                 cw_t = stage.tile([P, J, P, 4], BF16, align_bytes=64)
                 cw_t_of[g] = cw_t
-            words = cw_t_of[g][:].bitcast(F32)[:, 2 * pair:2 * pair + 2, :, :]
-            bank = banks_of[(g, pair)][:].rearrange("q u i l -> q i l u")
-            if on_scalar:
-                nc.scalar.copy(out=words, in_=bank)
-            else:
-                nc.vector.tensor_copy(out=words, in_=bank)
+            nc.vector.tensor_copy(out=cw_t_of[g][:].bitcast(F32)[:, 2 * pair:2 * pair + 2, :, :],
+                                  in_=banks_of[(g, pair)][:].rearrange("q u i l -> q i l u"))
 
         def quantise(g):
             if not is_group(g):
@@ -150,7 +146,7 @@ def tile_softmoe_pb_t_e_kernel(tc, h, w2_words, w2_scales, b2, logits, out):
                                   in_=cw_t_of[g][:].rearrange("q j l t -> q (j l t)"))
             codes_of[g], scales_of[g] = codes, scales
 
-        def front(s, copies_on_scalar):
+        def front(s):
             load(s + LOAD_AHEAD)
             transposes(s - 1)
             fold_max(s + 2, 0)
@@ -159,14 +155,15 @@ def tile_softmoe_pb_t_e_kernel(tc, h, w2_words, w2_scales, b2, logits, out):
             invert_sum(s)
             normalise(s)
             fold_max(s + 2, 2)
-            copy_out(s - 1, 0, copies_on_scalar)
+            copy_out(s - 1, 0)
             finish_max(s + 2)
-            copy_out(s - 1, 1, copies_on_scalar)
+            copy_out(s - 1, 1)
             exps(s + 1)
 
         def combine(g, outs):
             b = g // GROUPS_PER_BATCH
             o = outs.tile([P, J, D], F32)
+            rows = out_rows[g * P * J:(g + 1) * P * J, :].rearrange("(p j) d -> p j d", j=J)
             for j in range(J):
                 acc = psum_mm.tile([P, D], F32, tag="bank_mm")
                 nc.tensor.matmul_mx(out=acc[:],
@@ -175,9 +172,12 @@ def tile_softmoe_pb_t_e_kernel(tc, h, w2_words, w2_scales, b2, logits, out):
                                     rhs=eo_codes[:, b, :].bitcast(FP8X4),
                                     rhs_scale=eo_scales[:, b, :],
                                     start=True, stop=True)
-                nc.scalar.copy(out=o[:, j, :], in_=acc[:])
-            rows = out_rows[g * P * J:(g + 1) * P * J, :]
-            nc.scalar.dma_start(out=rows.rearrange("(p j) d -> p j d", j=J), in_=o[:])
+                if j == J - 1:
+                    nc.vector.tensor_copy(out=o[:, j, :], in_=acc[:])
+                else:
+                    nc.scalar.copy(out=o[:, j, :], in_=acc[:])
+                if j % 2 == 1:
+                    nc.sync.dma_start(out=rows[:, j - 1:j + 1, :], in_=o[:, j - 1:j + 1, :])
 
         with tc.tile_pool(name="experts", bufs=1) as experts:
             w2_planes = experts.tile([P, E, D], U8, align_bytes=64)
@@ -210,7 +210,7 @@ def tile_softmoe_pb_t_e_kernel(tc, h, w2_words, w2_scales, b2, logits, out):
                                           in_=w2_words_by_p[:, e0:e0 + 4, :])
 
                 for s in range(FIRST_STEP, H_STEP):
-                    front(s, False)
+                    front(s)
 
                 b2_bank = psum_mm.tile([P, D_CHUNKS, P], BF16, tag="bank_mm")
                 for c in range(D_CHUNKS):
@@ -219,7 +219,7 @@ def tile_softmoe_pb_t_e_kernel(tc, h, w2_words, w2_scales, b2, logits, out):
 
                 h_t_words = h_t[:].bitcast(F32)
                 for half in range(2):
-                    front(H_STEP + half, False)
+                    front(H_STEP + half)
                     some = slice(8 * half, 8 * half + 8)
                     for b in range(B):
                         bank = psum_mm.tile([P, 2, 2, P], F32, tag="bank_mm")
@@ -239,7 +239,7 @@ def tile_softmoe_pb_t_e_kernel(tc, h, w2_words, w2_scales, b2, logits, out):
                 eo_k = eo_stage.tile([P, B, D, 4], BF16, align_bytes=64)
 
                 for quarter in range(4):
-                    front(W_STEP + quarter, True)
+                    front(W_STEP + quarter)
                     for e in range(4 * quarter, 4 * quarter + 4):
                         acc = psum_mm.tile([P, D_CHUNKS, B * S], F32, tag="bank_mm")
                         for c in range(D_CHUNKS):
@@ -249,15 +249,14 @@ def tile_softmoe_pb_t_e_kernel(tc, h, w2_words, w2_scales, b2, logits, out):
                                                 rhs=h_codes[:, e, :].bitcast(FP8X4),
                                                 rhs_scale=h_scales[:, e, :],
                                                 start=True, stop=True)
-                        nc.vector.tensor_tensor(
-                            out=eo_t[:, :, :, e, :],
-                            in0=acc[:].rearrange("p c (b s) -> p c b s", s=S),
-                            in1=b2_t[:, :, e:e + 1].unsqueeze(3).to_broadcast([P, D_CHUNKS, B, S]),
-                            op=ALU.add)
+                        for c in range(D_CHUNKS):
+                            nc.scalar.activation(out=eo_t[:, c, :, e, :],
+                                                 in_=acc[:, c, :].rearrange("p (b s) -> p b s", s=S),
+                                                 func=ACT.Identity, bias=b2_t[:, c, e:e + 1], scale=1.0)
 
                 eo_k_words = eo_k[:].bitcast(F32)
                 for pair in range(2):
-                    front(EO_STEP + pair, False)
+                    front(EO_STEP + pair)
                     for b in (2 * pair, 2 * pair + 1):
                         for half in range(2):
                             bank = psum_mm.tile([P, 2, 2 * P], F32, tag="bank_mm")
@@ -276,7 +275,7 @@ def tile_softmoe_pb_t_e_kernel(tc, h, w2_words, w2_scales, b2, logits, out):
         with tc.tile_pool(name="outs", bufs=4) as outs:
             combined = 0
             for s in range(OUT_STEP, LAST_STEP + 1):
-                front(s, False)
+                front(s)
                 for n in range(2):
                     if combined <= s - 2:
                         combine(combined, outs)

@@ -17,7 +17,7 @@ J = 4
 GROUPS = B * L // (P * J)
 GROUPS_PER_BATCH = GROUPS // B
 D_CHUNKS = D // P
-FOLDS = 3
+FOLDS = 2
 LOAD_AHEAD = 4
 
 FIRST_STEP = -2
@@ -154,7 +154,6 @@ def tile_softmoe_pb_t_e_kernel(tc, h, w2_words, w2_scales, b2, logits, out):
             fold_max(s + 2, 1)
             invert_sum(s)
             normalise(s)
-            fold_max(s + 2, 2)
             copy_out(s - 1, 0)
             finish_max(s + 2)
             copy_out(s - 1, 1)

@@ -22,9 +22,9 @@ LOAD_AHEAD = 4
 
 FIRST_STEP = -2
 H_STEP = 1
-W_STEP = H_STEP + 2
-EO_STEP = W_STEP + 4
-OUT_STEP = EO_STEP + 2
+W_STEP = H_STEP + 1
+EO_STEP = W_STEP + 2
+OUT_STEP = EO_STEP + 1
 LAST_STEP = GROUPS + 1
 
 FLOPS = 2 * B * E * S * H * D + 2 * B * L * K * D
@@ -42,7 +42,7 @@ def tile_softmoe_pb_t_e_kernel(tc, h, w2_words, w2_scales, b2, logits, out):
             tc.tile_pool(name="xs", bufs=6) as xs, \
             tc.tile_pool(name="work", bufs=3) as work, \
             tc.tile_pool(name="stage", bufs=2) as stage, \
-            tc.tile_pool(name="cwq", bufs=10) as cwq, \
+            tc.tile_pool(name="cwq", bufs=8) as cwq, \
             tc.psum_pool(name="psum_t", bufs=4) as psum_t, \
             tc.psum_pool(name="psum_mm", bufs=4) as psum_mm:
 
@@ -112,9 +112,14 @@ def tile_softmoe_pb_t_e_kernel(tc, h, w2_words, w2_scales, b2, logits, out):
                 return
             cw = work.tile([P, J, K], BF16)
             for j in range(J):
-                nc.gpsimd.tensor_scalar(out=cw[:, j, :], in0=ex_of[g][:, j, :],
-                                        scalar1=inv_sum_of[g][:, j:j + 1], scalar2=0.0,
-                                        op0=ALU.mult, op1=ALU.add)
+                if j % 2 == 0:
+                    nc.gpsimd.tensor_scalar(out=cw[:, j, :], in0=ex_of[g][:, j, :],
+                                            scalar1=inv_sum_of[g][:, j:j + 1], scalar2=0.0,
+                                            op0=ALU.mult, op1=ALU.add)
+                else:
+                    nc.vector.tensor_scalar(out=cw[:, j, :], in0=ex_of[g][:, j, :],
+                                            scalar1=inv_sum_of[g][:, j:j + 1], scalar2=None,
+                                            op0=ALU.mult)
             cw_of[g] = cw
 
         def transposes(g):
@@ -171,10 +176,7 @@ def tile_softmoe_pb_t_e_kernel(tc, h, w2_words, w2_scales, b2, logits, out):
                                     rhs=eo_codes[:, b, :].bitcast(FP8X4),
                                     rhs_scale=eo_scales[:, b, :],
                                     start=True, stop=True)
-                if j == J - 1:
-                    nc.vector.tensor_copy(out=o[:, j, :], in_=acc[:])
-                else:
-                    nc.scalar.copy(out=o[:, j, :], in_=acc[:])
+                nc.scalar.copy(out=o[:, j, :], in_=acc[:])
                 if j % 2 == 1:
                     nc.sync.dma_start(out=rows[:, j - 1:j + 1, :], in_=o[:, j - 1:j + 1, :])
 
@@ -217,8 +219,8 @@ def tile_softmoe_pb_t_e_kernel(tc, h, w2_words, w2_scales, b2, logits, out):
                 nc.scalar.copy(out=b2_t[:], in_=b2_bank[:, :, 0:E])
 
                 h_t_words = h_t[:].bitcast(F32)
+                front(H_STEP)
                 for half in range(2):
-                    front(H_STEP + half)
                     some = slice(8 * half, 8 * half + 8)
                     for b in range(B):
                         bank = psum_mm.tile([P, 2, 2, P], F32, tag="bank_mm")
@@ -237,9 +239,9 @@ def tile_softmoe_pb_t_e_kernel(tc, h, w2_words, w2_scales, b2, logits, out):
                 eo_t = eo_stage.tile([P, D_CHUNKS, B, E, S], BF16)
                 eo_k = eo_stage.tile([P, B, D, 4], BF16, align_bytes=64)
 
-                for quarter in range(4):
-                    front(W_STEP + quarter)
-                    for e in range(4 * quarter, 4 * quarter + 4):
+                for half in range(2):
+                    front(W_STEP + half)
+                    for e in range(8 * half, 8 * half + 8):
                         acc = psum_mm.tile([P, D_CHUNKS, B * S], F32, tag="bank_mm")
                         for c in range(D_CHUNKS):
                             nc.tensor.matmul_mx(out=acc[:, c, :],
@@ -254,22 +256,20 @@ def tile_softmoe_pb_t_e_kernel(tc, h, w2_words, w2_scales, b2, logits, out):
                                                  func=ACT.Identity, bias=b2_t[:, c, e:e + 1], scale=1.0)
 
                 eo_k_words = eo_k[:].bitcast(F32)
-                for pair in range(2):
-                    front(EO_STEP + pair)
-                    for b in (2 * pair, 2 * pair + 1):
-                        for half in range(2):
-                            bank = psum_mm.tile([P, 2, 2 * P], F32, tag="bank_mm")
-                            for i in range(2):
-                                words = eo_t[:, 2 * half + i, b, :, :].rearrange("p e s -> p (e s)").bitcast(F32)
-                                for u in range(2):
-                                    nc.tensor.transpose(bank[:, u, i * P:(i + 1) * P],
-                                                        words[:, u * P:(u + 1) * P], ident_f32[:])
-                            nc.scalar.copy(out=eo_k_words[:, b, 2 * half * P:2 * (half + 1) * P, :],
-                                           in_=bank[:].rearrange("q u d -> q d u"))
-                    for b in (2 * pair, 2 * pair + 1):
-                        nc.vector.quantize_mx(out=eo_codes[:, b, :].bitcast(FP8X4),
-                                              scales=eo_scales[:, b, :],
-                                              in_=eo_k[:, b, :, :].rearrange("q d t -> q (d t)"))
+                front(EO_STEP)
+                for b in range(B):
+                    for half in range(2):
+                        bank = psum_mm.tile([P, 2, 2 * P], F32, tag="bank_mm")
+                        for i in range(2):
+                            words = eo_t[:, 2 * half + i, b, :, :].rearrange("p e s -> p (e s)").bitcast(F32)
+                            for u in range(2):
+                                nc.tensor.transpose(bank[:, u, i * P:(i + 1) * P],
+                                                    words[:, u * P:(u + 1) * P], ident_f32[:])
+                        nc.scalar.copy(out=eo_k_words[:, b, 2 * half * P:2 * (half + 1) * P, :],
+                                       in_=bank[:].rearrange("q u d -> q d u"))
+                    nc.vector.quantize_mx(out=eo_codes[:, b, :].bitcast(FP8X4),
+                                          scales=eo_scales[:, b, :],
+                                          in_=eo_k[:, b, :, :].rearrange("q d t -> q (d t)"))
 
         with tc.tile_pool(name="outs", bufs=4) as outs:
             combined = 0

@@ -17,15 +17,16 @@ J = 4
 GROUPS = B * L // (P * J)
 GROUPS_PER_BATCH = GROUPS // B
 D_CHUNKS = D // P
+T = 4
+Q = E // T
 FOLDS = 2
 LOAD_AHEAD = 4
+PITCH = T * P + S
 
 FIRST_STEP = -2
-H_STEP = 1
-W_STEP = H_STEP + 1
-EO_STEP = W_STEP + 2
-OUT_STEP = EO_STEP + 1
+EO_STEP = 2
 LAST_STEP = GROUPS + 1
+LAG = 4
 
 FLOPS = 2 * B * E * S * H * D + 2 * B * L * K * D
 
@@ -43,19 +44,27 @@ def tile_softmoe_pb_t_e_kernel(tc, h, w2_words, w2_scales, b2, logits, out):
             tc.tile_pool(name="work", bufs=3) as work, \
             tc.tile_pool(name="stage", bufs=2) as stage, \
             tc.tile_pool(name="cwq", bufs=8) as cwq, \
-            tc.psum_pool(name="psum_t", bufs=4) as psum_t, \
+            tc.tile_pool(name="outs", bufs=6) as outs, \
+            tc.psum_pool(name="psum_t", bufs=2) as psum_t, \
+            tc.psum_pool(name="psum_e", bufs=2) as psum_e, \
             tc.psum_pool(name="psum_mm", bufs=4) as psum_mm:
 
         ident_f32 = const.tile([P, P], F32)
         make_identity(nc, ident_f32[:])
-        ident_bf16 = const.tile([P, P], BF16)
-        nc.vector.tensor_copy(out=ident_bf16[:], in_=ident_f32[:])
         warm = const.tile([P, 1], F32)
         nc.vector.memset(warm[:], 0.0)
         nc.scalar.activation(out=warm[:], in_=warm[:], func=ACT.Exp)
 
         eo_codes = const.tile([P, B, D], U32, align_bytes=64)
         eo_scales = const.tile([P, B, D], U8, align_bytes=64)
+        w2_planes = const.tile([P, E, D], U8, align_bytes=64)
+        w2_codes = const.tile([P, E, D], U32, align_bytes=64)
+        h_rows = const.tile([P, B * T, H], BF16)
+        h_scales = const.tile([P, B, T * P], U8, align_bytes=64)
+        b2_rows = const.tile([P, T, D], BF16)
+        padded = [const.tile([P, Q * PITCH], U32, align_bytes=64, name="padded%d" % i) for i in range(2)]
+        nc.vector.memset(w2_planes[:].bitcast(I32), 0)
+        nc.vector.memset(padded[0][:].bitcast(I32), 0)
 
         x_of, folded, neg_max_of, ex_of, ex_sum_of, inv_sum_of = {}, {}, {}, {}, {}, {}
         cw_of, banks_of, cw_t_of, codes_of, scales_of = {}, {}, {}, {}, {}
@@ -89,16 +98,19 @@ def tile_softmoe_pb_t_e_kernel(tc, h, w2_words, w2_scales, b2, logits, out):
                                     axis=mybir.AxisListType.X, op=ALU.max, negate=True)
             neg_max_of[g] = neg_max
 
-        def exps(g):
+        def exps(g, tiles):
             if not is_group(g):
                 return
-            ex = work.tile([P, J, K], F32)
-            ex_sum = small.tile([P, J], F32)
-            for j in range(J):
-                nc.scalar.activation(out=ex[:, j, :], in_=x_of[g][:, j, :], func=ACT.Exp,
+            if g not in ex_of:
+                ex = work.tile([P, J, K], F32)
+                ex_sum = small.tile([P, J], F32)
+                ex_of[g], ex_sum_of[g] = ex, ex_sum
+            for j in tiles:
+                nc.scalar.activation(out=ex_of[g][:, j, :].rearrange("p (u q e) -> p u q e", u=2, e=2),
+                                     in_=x_of[g][:, j, :].rearrange("p (u e q) -> p u q e", u=2, e=2),
+                                     func=ACT.Exp,
                                      bias=neg_max_of[g][:, j:j + 1], scale=1.0,
-                                     accum_out=ex_sum[:, j:j + 1])
-            ex_of[g], ex_sum_of[g] = ex, ex_sum
+                                     accum_out=ex_sum_of[g][:, j:j + 1])
 
         def invert_sum(g):
             if not is_group(g):
@@ -112,14 +124,9 @@ def tile_softmoe_pb_t_e_kernel(tc, h, w2_words, w2_scales, b2, logits, out):
                 return
             cw = work.tile([P, J, K], BF16)
             for j in range(J):
-                if j % 2 == 0:
-                    nc.gpsimd.tensor_scalar(out=cw[:, j, :], in0=ex_of[g][:, j, :],
-                                            scalar1=inv_sum_of[g][:, j:j + 1], scalar2=0.0,
-                                            op0=ALU.mult, op1=ALU.add)
-                else:
-                    nc.vector.tensor_scalar(out=cw[:, j, :], in0=ex_of[g][:, j, :],
-                                            scalar1=inv_sum_of[g][:, j:j + 1], scalar2=None,
-                                            op0=ALU.mult)
+                nc.gpsimd.tensor_scalar(out=cw[:, j, :], in0=ex_of[g][:, j, :],
+                                        scalar1=inv_sum_of[g][:, j:j + 1], scalar2=0.0,
+                                        op0=ALU.mult, op1=ALU.add)
             cw_of[g] = cw
 
         def transposes(g):
@@ -133,14 +140,15 @@ def tile_softmoe_pb_t_e_kernel(tc, h, w2_words, w2_scales, b2, logits, out):
                         nc.tensor.transpose(bank[:, u, i, :], words[:, u * P:(u + 1) * P], ident_f32[:])
                 banks_of[(g, pair)] = bank
 
-        def copy_out(g, pair):
+        def copy_out(g, pair, on_scalar):
             if not is_group(g):
                 return
             if pair == 0:
                 cw_t = stage.tile([P, J, P, 4], BF16, align_bytes=64)
                 cw_t_of[g] = cw_t
-            nc.vector.tensor_copy(out=cw_t_of[g][:].bitcast(F32)[:, 2 * pair:2 * pair + 2, :, :],
-                                  in_=banks_of[(g, pair)][:].rearrange("q u i l -> q i l u"))
+            copy = nc.scalar.copy if on_scalar else nc.vector.tensor_copy
+            copy(out=cw_t_of[g][:].bitcast(F32)[:, 2 * pair:2 * pair + 2, :, :],
+                 in_=banks_of[(g, pair)][:].rearrange("q u i l -> q i l u"))
 
         def quantise(g):
             if not is_group(g):
@@ -151,23 +159,65 @@ def tile_softmoe_pb_t_e_kernel(tc, h, w2_words, w2_scales, b2, logits, out):
                                   in_=cw_t_of[g][:].rearrange("q j l t -> q (j l t)"))
             codes_of[g], scales_of[g] = codes, scales
 
-        def front(s):
-            load(s + LOAD_AHEAD)
-            transposes(s - 1)
-            fold_max(s + 2, 0)
-            quantise(s - 2)
-            fold_max(s + 2, 1)
-            invert_sum(s)
-            normalise(s)
-            copy_out(s - 1, 0)
-            finish_max(s + 2)
-            copy_out(s - 1, 1)
-            exps(s + 1)
+        h_t_of, h_codes_of, eo_banks, eo_k_of = {}, {}, {}, {}
 
-        def combine(g, outs):
+        def turn_h(b):
+            h_t = stage.tile([P, T * P, 4], BF16, align_bytes=64)
+            h_t_words = h_t[:].bitcast(F32).rearrange("p (t m) u -> p t m u", m=P)
+            for half in range(2):
+                bank = psum_mm.tile([P, 2, 2, P], F32, tag="bank_mm")
+                for i in range(2):
+                    words = h_rows[:, T * b + 2 * half + i, :].bitcast(F32)
+                    for u in range(2):
+                        nc.tensor.transpose(bank[:, u, i, :], words[:, u:H // 2:2], ident_f32[:])
+                nc.scalar.copy(out=h_t_words[:, 2 * half:2 * half + 2, :, :],
+                               in_=bank[:].rearrange("p u i m -> p i m u"))
+            h_t_of[b] = h_t
+
+        def quantise_h(b):
+            h_codes = stage.tile([P, T * P], U32, align_bytes=64)
+            nc.vector.quantize_mx(out=h_codes[:].bitcast(FP8X4), scales=h_scales[:, b, :],
+                                  in_=h_t_of[b][:].rearrange("p m t -> p (m t)"))
+            h_codes_of[b] = h_codes
+
+        def spread(b):
+            own = padded[b % 2][:].rearrange("p (q w) -> p q w", q=Q)[:, :, 0:T * P]
+            own = own.rearrange("p q (t m) -> p q t m", m=P)[:, :, :, 0:S]
+            nc.vector.tensor_copy(out=own.bitcast(I32),
+                                  in_=h_codes_of[b][:].rearrange("p (t q s) -> p q t s", t=T, q=Q).bitcast(I32))
+
+        def open_eo(b, c):
+            pool, tag = (psum_mm, "bank_mm") if b == 0 else (psum_e, "bank_e")
+            bank = pool.tile([P, T, P], F32, tag=tag)
+            eo_banks[(b, c)] = bank
+
+        def multiply_eo(b, c, t):
+            for q in range(Q):
+                at = q * T * P + t * P
+                nc.tensor.matmul_mx(out=eo_banks[(b, c)][:, t, :],
+                                    lhsT=padded[b % 2][:, at:at + P].bitcast(FP8X4),
+                                    lhsT_scale=h_scales[:, b, t * P:(t + 1) * P],
+                                    rhs=w2_codes[:, Q * t + q, c * P:(c + 1) * P].bitcast(FP8X4),
+                                    rhs_scale=w2_planes[:, Q * t + q, c * P:(c + 1) * P],
+                                    start=(q == 0), stop=(q == Q - 1))
+
+        def add_b2(b, c):
+            if c == 0:
+                eo_k = stage.tile([P, D, T], BF16, align_bytes=64)
+                eo_k_of[b] = eo_k
+            d = slice(c * P, (c + 1) * P)
+            nc.vector.tensor_tensor(out=eo_k_of[b][:, d, :],
+                                    in0=eo_banks[(b, c)][:].rearrange("m t d -> m d t"),
+                                    in1=b2_rows[:, :, d].rearrange("m t d -> m d t"), op=ALU.add)
+
+        def quantise_eo(b):
+            nc.vector.quantize_mx(out=eo_codes[:, b, :].bitcast(FP8X4), scales=eo_scales[:, b, :],
+                                  in_=eo_k_of[b][:].rearrange("m d t -> m (d t)"))
+
+        acc_of, o_of = {}, {}
+
+        def combine(g):
             b = g // GROUPS_PER_BATCH
-            o = outs.tile([P, J, D], F32)
-            rows = out_rows[g * P * J:(g + 1) * P * J, :].rearrange("(p j) d -> p j d", j=J)
             for j in range(J):
                 acc = psum_mm.tile([P, D], F32, tag="bank_mm")
                 nc.tensor.matmul_mx(out=acc[:],
@@ -176,106 +226,108 @@ def tile_softmoe_pb_t_e_kernel(tc, h, w2_words, w2_scales, b2, logits, out):
                                     rhs=eo_codes[:, b, :].bitcast(FP8X4),
                                     rhs_scale=eo_scales[:, b, :],
                                     start=True, stop=True)
-                nc.scalar.copy(out=o[:, j, :], in_=acc[:])
-                if j % 2 == 1:
-                    nc.sync.dma_start(out=rows[:, j - 1:j + 1, :], in_=o[:, j - 1:j + 1, :])
+                acc_of[(g, j)] = acc
 
-        with tc.tile_pool(name="experts", bufs=1) as experts:
-            w2_planes = experts.tile([P, E, D], U8, align_bytes=64)
-            w2_codes = experts.tile([P, E, D], U32, align_bytes=64)
-            h_codes = experts.tile([P, E, B * S], U32, align_bytes=64)
-            h_scales = experts.tile([P, E, B * S], U8, align_bytes=64)
-            b2_rows = experts.tile([P, D], BF16)
-            b2_t = experts.tile([P, D_CHUNKS, E], F32)
-            nc.vector.memset(w2_planes[:].bitcast(I32), 0)
-            nc.vector.memset(b2_rows[:], 0.0)
+        def take_out(g, j, copy):
+            if j % 2 == 0:
+                o = outs.tile([P, 2, D], F32)
+                o_of[(g, j // 2)] = o
+            copy(out=o_of[(g, j // 2)][:, j % 2, :], in_=acc_of[(g, j)][:])
 
-            with tc.tile_pool(name="h_stage", bufs=1) as h_stage:
-                h_rows = h_stage.tile([P, B * E * S // P, H], BF16)
-                h_t = h_stage.tile([P, E, B, S, 4], BF16, align_bytes=64)
+        def store(g, half):
+            rows = out_rows[g * P * J:(g + 1) * P * J, :].rearrange("(p j) d -> p j d", j=J)
+            nc.sync.dma_start(out=rows[:, 2 * half:2 * half + 2, :], in_=o_of[(g, half)][:])
 
-                for g in range(3):
-                    load(g)
-                nc.sync.dma_start(out=h_rows[:],
-                                  in_=h.rearrange("b e s k -> (b e s) k").rearrange("(n p) k -> p n k", p=P))
-                scale_rows = w2_scales.rearrange("g (qq r) n -> r qq g n", r=4)
-                for r in range(4):
-                    nc.sync.dma_start(out=w2_planes[r:P:32, :, :].bitcast(I32),
-                                      in_=scale_rows[r].bitcast(I32))
-                nc.sync.dma_start(out=b2_rows[0:E, :], in_=b2)
-                w2_words_by_p = w2_words.rearrange("g p n t -> p g (n t)").bitcast(I32)
+        h_by_tile = h.rearrange("b e s k -> (b e s) k").rearrange("(n p) k -> p n k", p=P)
+        scale_rows = w2_scales.rearrange("g (qq r) n -> r qq g n", r=4)
+        w2_words_by_p = w2_words.rearrange("g p n t -> p g (n t)").bitcast(I32)
+        b2_by_q = b2.rearrange("(t q) d -> q t d", q=Q)
+
+        def load_h(first, last):
+            nc.sync.dma_start(out=h_rows[:, T * first:T * last, :], in_=h_by_tile[:, T * first:T * last, :])
+
+        def load_w2(t):
+            nc.sync.dma_start(out=w2_codes[:, Q * t:Q * t + Q, :].bitcast(I32),
+                              in_=w2_words_by_p[:, Q * t:Q * t + Q, :])
+
+        load(0)
+        load(1)
+        load_h(0, 2)
+        load(2)
+        load(3)
+        for r in range(4):
+            nc.sync.dma_start(out=w2_planes[r:P:32, :, :].bitcast(I32), in_=scale_rows[r].bitcast(I32))
+        load_w2(0)
+        load_w2(1)
+        load(4)
+        load_w2(2)
+        load_w2(3)
+        for q in range(Q):
+            nc.sync.dma_start(out=b2_rows[S * q:S * q + S, :, :], in_=b2_by_q[q].partition_broadcast(S))
+        load_h(2, 4)
+
+        TURN = {0: 0, 1: 1, 2: 3, 3: 5}
+        MULTIPLY = {2: [(0, 0), (0, 1), (0, 2), (0, 3)], 3: [(1, 0), (1, 1)], 4: [(1, 2), (1, 3)]}
+        for b in range(2, B):
+            for c in range(D_CHUNKS):
+                MULTIPLY[4 * b - 3 + c] = [(b, c)]
+
+        added = -1
+        made = -1
+        combined = 0
+        pending = []
+        for s in range(FIRST_STEP, LAST_STEP + 1):
+            draining = s >= GROUPS
+            load(s + LOAD_AHEAD)
+
+            if added > made:
+                quantise_eo(added)
+                made = added
+            quantise(s - 2)
+            fold_max(s + 2, 0)
+            fold_max(s + 2, 1)
+            for b in range(B):
+                if s == TURN[b] + 1:
+                    quantise_h(b)
+                    spread(b)
+            invert_sum(s)
+            normalise(s)
+
+            transposes(s - 1)
+            top = s - LAG if s < GROUPS - 1 else s - 2 if draining else s - 3
+            ready = [g for g in range(combined, GROUPS) if g <= top and g // GROUPS_PER_BATCH <= made][:2]
+            combined += len(ready)
+            for g in ready:
+                combine(g)
+            exps(s + 1, range(0, 2))
+            copy_out(s - 1, 0, False)
+            for b, c in pending:
+                add_b2(b, c)
+                if c == D_CHUNKS - 1:
+                    added = b
+            pending = []
+            finish_max(s + 2)
+            copy_out(s - 1, 1, len(ready) == 0)
+            for i, g in enumerate(ready):
                 for half in range(2):
-                    load(3 + half)
-                    for e0 in (8 * half, 8 * half + 4):
-                        nc.sync.dma_start(out=w2_codes[:, e0:e0 + 4, :].bitcast(I32),
-                                          in_=w2_words_by_p[:, e0:e0 + 4, :])
-
-                for s in range(FIRST_STEP, H_STEP):
-                    front(s)
-
-                b2_bank = psum_mm.tile([P, D_CHUNKS, P], BF16, tag="bank_mm")
-                for c in range(D_CHUNKS):
-                    nc.tensor.transpose(b2_bank[:, c, :], b2_rows[:, c * P:(c + 1) * P], ident_bf16[:])
-                nc.scalar.copy(out=b2_t[:], in_=b2_bank[:, :, 0:E])
-
-                h_t_words = h_t[:].bitcast(F32)
-                front(H_STEP)
-                for half in range(2):
-                    some = slice(8 * half, 8 * half + 8)
-                    for b in range(B):
-                        bank = psum_mm.tile([P, 2, 2, P], F32, tag="bank_mm")
-                        for i in range(2):
-                            words = h_rows[:, 4 * b + 2 * half + i, :].bitcast(F32)
-                            for u in range(2):
-                                nc.tensor.transpose(bank[:, u, i, :], words[:, u:H // 2:2], ident_f32[:])
-                        nc.scalar.copy(out=h_t_words[:, some, b, :, :],
-                                       in_=bank[:].rearrange("p u i (q s) -> p (i q) s u", s=S))
-                    nc.vector.quantize_mx(
-                        out=h_codes[:, some, :].rearrange("p e m -> p (e m)").bitcast(FP8X4),
-                        scales=h_scales[:, some, :].rearrange("p e m -> p (e m)"),
-                        in_=h_t[:, some, :, :, :].rearrange("p e b s t -> p (e b s t)"))
-
-            with tc.tile_pool(name="eo_stage", bufs=1) as eo_stage:
-                eo_t = eo_stage.tile([P, D_CHUNKS, B, E, S], BF16)
-                eo_k = eo_stage.tile([P, B, D, 4], BF16, align_bytes=64)
-
-                for half in range(2):
-                    front(W_STEP + half)
-                    for e in range(8 * half, 8 * half + 8):
-                        acc = psum_mm.tile([P, D_CHUNKS, B * S], F32, tag="bank_mm")
-                        for c in range(D_CHUNKS):
-                            nc.tensor.matmul_mx(out=acc[:, c, :],
-                                                lhsT=w2_codes[:, e, c * P:(c + 1) * P].bitcast(FP8X4),
-                                                lhsT_scale=w2_planes[:, e, c * P:(c + 1) * P],
-                                                rhs=h_codes[:, e, :].bitcast(FP8X4),
-                                                rhs_scale=h_scales[:, e, :],
-                                                start=True, stop=True)
-                        for c in range(D_CHUNKS):
-                            nc.scalar.activation(out=eo_t[:, c, :, e, :],
-                                                 in_=acc[:, c, :].rearrange("p (b s) -> p b s", s=S),
-                                                 func=ACT.Identity, bias=b2_t[:, c, e:e + 1], scale=1.0)
-
-                eo_k_words = eo_k[:].bitcast(F32)
-                front(EO_STEP)
-                for b in range(B):
-                    for half in range(2):
-                        bank = psum_mm.tile([P, 2, 2 * P], F32, tag="bank_mm")
-                        for i in range(2):
-                            words = eo_t[:, 2 * half + i, b, :, :].rearrange("p e s -> p (e s)").bitcast(F32)
-                            for u in range(2):
-                                nc.tensor.transpose(bank[:, u, i * P:(i + 1) * P],
-                                                    words[:, u * P:(u + 1) * P], ident_f32[:])
-                        nc.scalar.copy(out=eo_k_words[:, b, 2 * half * P:2 * (half + 1) * P, :],
-                                       in_=bank[:].rearrange("q u d -> q d u"))
-                    nc.vector.quantize_mx(out=eo_codes[:, b, :].bitcast(FP8X4),
-                                          scales=eo_scales[:, b, :],
-                                          in_=eo_k[:, b, :, :].rearrange("q d t -> q (d t)"))
-
-        with tc.tile_pool(name="outs", bufs=4) as outs:
-            combined = 0
-            for s in range(OUT_STEP, LAST_STEP + 1):
-                front(s)
-                for n in range(2):
-                    if combined <= s - 2:
-                        combine(combined, outs)
-                        combined += 1
+                    for j in (2 * half, 2 * half + 1):
+                        on_vector = (j == 3 and g % 4 == 3) or (s >= GROUPS - 1 and j % 2 == 1)
+                        take_out(g, j, nc.vector.tensor_copy if on_vector else nc.scalar.copy)
+                    store(g, half)
+                    if i == 0 and half == 0:
+                        exps(s + 1, range(2, 4))
+            if not ready:
+                exps(s + 1, range(2, 4))
+            todo = MULTIPLY.get(s, [])
+            for b, c in todo:
+                open_eo(b, c)
+            for t in range(T):
+                for b, c in todo:
+                    multiply_eo(b, c, t)
+            pending = todo
+            for b in range(B):
+                if s == TURN[b]:
+                    turn_h(b)
+            if s == -1:
+                nc.vector.memset(padded[1][:].bitcast(I32), 0)
+        assert combined == GROUPS

@@ -119,15 +119,16 @@ def tile_softmoe_pb_t_e_kernel(tc, h, w2_words, w2_scales, b2, logits, out):
             nc.vector.reciprocal(out=inv_sum[:], in_=ex_sum_of[g][:])
             inv_sum_of[g] = inv_sum
 
-        def normalise(g):
+        def normalise(g, tiles, engine):
             if not is_group(g):
                 return
-            cw = work.tile([P, J, K], BF16)
-            for j in range(J):
-                nc.gpsimd.tensor_scalar(out=cw[:, j, :], in0=ex_of[g][:, j, :],
-                                        scalar1=inv_sum_of[g][:, j:j + 1], scalar2=0.0,
-                                        op0=ALU.mult, op1=ALU.add)
-            cw_of[g] = cw
+            if g not in cw_of:
+                cw = work.tile([P, J, K], BF16)
+                cw_of[g] = cw
+            for j in tiles:
+                engine.tensor_scalar(out=cw_of[g][:, j, :], in0=ex_of[g][:, j, :],
+                                     scalar1=inv_sum_of[g][:, j:j + 1], scalar2=0.0,
+                                     op0=ALU.mult, op1=ALU.add)
 
         def transposes(g):
             if not is_group(g):
@@ -262,15 +263,18 @@ def tile_softmoe_pb_t_e_kernel(tc, h, w2_words, w2_scales, b2, logits, out):
         load(4)
         load_w2(2)
         load_w2(3)
+        load(5)
         for q in range(Q):
             nc.sync.dma_start(out=b2_rows[S * q:S * q + S, :, :], in_=b2_by_q[q].partition_broadcast(S))
         load_h(2, 4)
 
-        TURN = {0: 0, 1: 1, 2: 3, 3: 5}
-        MULTIPLY = {2: [(0, 0), (0, 1), (0, 2), (0, 3)], 3: [(1, 0), (1, 1)], 4: [(1, 2), (1, 3)]}
+        TURN = {0: 0, 1: 1, 3: 2, 5: 3}
+        MULTIPLY = {1: [(0, c, t) for t in (0, 1) for c in range(D_CHUNKS)],
+                    2: [(0, c, t) for t in (2, 3) for c in range(D_CHUNKS)],
+                    3: [(1, 0, t) for t in range(T)], 4: [(1, c, t) for c in (1, 2) for t in range(T)], 5: [(1, 3, t) for t in range(T)]}
         for b in range(2, B):
             for c in range(D_CHUNKS):
-                MULTIPLY[4 * b - 3 + c] = [(b, c)]
+                MULTIPLY[4 * b - 2 + c] = [(b, c, t) for t in range(T)]
 
         added = -1
         made = -1
@@ -283,16 +287,14 @@ def tile_softmoe_pb_t_e_kernel(tc, h, w2_words, w2_scales, b2, logits, out):
             if added > made:
                 quantise_eo(added)
                 made = added
-            quantise(s - 2)
             fold_max(s + 2, 0)
+            quantise(s - 2)
             fold_max(s + 2, 1)
-            for b in range(B):
-                if s == TURN[b] + 1:
-                    quantise_h(b)
-                    spread(b)
+            if s - 1 in TURN:
+                quantise_h(TURN[s - 1])
+                spread(TURN[s - 1])
             invert_sum(s)
-            normalise(s)
-
+            normalise(s, range(2, J), nc.gpsimd)
             transposes(s - 1)
             top = s - LAG if s < GROUPS - 1 else s - 2 if draining else s - 3
             ready = [g for g in range(combined, GROUPS) if g <= top and g // GROUPS_PER_BATCH <= made][:2]
@@ -308,26 +310,25 @@ def tile_softmoe_pb_t_e_kernel(tc, h, w2_words, w2_scales, b2, logits, out):
             pending = []
             finish_max(s + 2)
             copy_out(s - 1, 1, len(ready) == 0)
+            normalise(s, range(0, 2), nc.vector)
             for i, g in enumerate(ready):
                 for half in range(2):
                     for j in (2 * half, 2 * half + 1):
-                        on_vector = (j == 3 and g % 4 == 3) or (s >= GROUPS - 1 and j % 2 == 1)
+                        on_vector = s >= GROUPS - 1 and j % 2 == 1
                         take_out(g, j, nc.vector.tensor_copy if on_vector else nc.scalar.copy)
                     store(g, half)
                     if i == 0 and half == 0:
                         exps(s + 1, range(2, 4))
             if not ready:
                 exps(s + 1, range(2, 4))
-            todo = MULTIPLY.get(s, [])
-            for b, c in todo:
-                open_eo(b, c)
-            for t in range(T):
-                for b, c in todo:
-                    multiply_eo(b, c, t)
-            pending = todo
-            for b in range(B):
-                if s == TURN[b]:
-                    turn_h(b)
+            if s in TURN:
+                turn_h(TURN[s])
+            for b, c, t in MULTIPLY.get(s, []):
+                if t == 0:
+                    open_eo(b, c)
+                multiply_eo(b, c, t)
+                if t == T - 1:
+                    pending.append((b, c))
             if s == -1:
                 nc.vector.memset(padded[1][:].bitcast(I32), 0)
         assert combined == GROUPS

@@ -61,10 +61,13 @@ def tile_softmoe_pb_t_e_kernel(tc, h, w2_words, w2_scales, b2, logits, out):
         w2_codes = const.tile([P, E, D], U32, align_bytes=64)
         h_rows = const.tile([P, B * T, H], BF16)
         h_scales = const.tile([P, B, T * P], U8, align_bytes=64)
-        b2_rows = const.tile([P, T, D], BF16)
+        b2_rows = const.tile([P, D], BF16)
+        pick = const.tile([P, T, P], BF16)
+        b2_wide = const.tile([P, D, T], BF16)
+        nc.vector.memset(b2_rows[:], 0.0)
         padded = [const.tile([P, Q * PITCH], U32, align_bytes=64, name="padded%d" % i) for i in range(2)]
+        nc.sync.dma_start(out=b2_rows[0:E, :], in_=b2)
         nc.vector.memset(w2_planes[:].bitcast(I32), 0)
-        nc.vector.memset(padded[0][:].bitcast(I32), 0)
 
         x_of, folded, neg_max_of, ex_of, ex_sum_of, inv_sum_of = {}, {}, {}, {}, {}, {}
         cw_of, banks_of, cw_t_of, codes_of, scales_of = {}, {}, {}, {}, {}
@@ -187,6 +190,16 @@ def tile_softmoe_pb_t_e_kernel(tc, h, w2_words, w2_scales, b2, logits, out):
             nc.vector.tensor_copy(out=own.bitcast(I32),
                                   in_=h_codes_of[b][:].rearrange("p (t q s) -> p q t s", t=T, q=Q).bitcast(I32))
 
+        def widen_b2():
+            nc.vector.tensor_copy(out=pick[:].rearrange("p t (q s) -> p (t q) s", s=S),
+                                  in_=ident_f32[:, 0:E].unsqueeze(2).to_broadcast([P, E, S]))
+            for c in range(D_CHUNKS):
+                bank = psum_mm.tile([P, T, P], F32, tag="bank_mm")
+                for t in range(T):
+                    nc.tensor.matmul(bank[:, t, :], lhsT=pick[:, t, :], rhs=b2_rows[:, c * P:(c + 1) * P],
+                                     start=True, stop=True)
+                nc.scalar.copy(out=b2_wide[:, c * P:(c + 1) * P, :], in_=bank[:].rearrange("m t d -> m d t"))
+
         def open_eo(b, c):
             pool, tag = (psum_mm, "bank_mm") if b == 0 else (psum_e, "bank_e")
             bank = pool.tile([P, T, P], F32, tag=tag)
@@ -209,7 +222,7 @@ def tile_softmoe_pb_t_e_kernel(tc, h, w2_words, w2_scales, b2, logits, out):
             d = slice(c * P, (c + 1) * P)
             nc.vector.tensor_tensor(out=eo_k_of[b][:, d, :],
                                     in0=eo_banks[(b, c)][:].rearrange("m t d -> m d t"),
-                                    in1=b2_rows[:, :, d].rearrange("m t d -> m d t"), op=ALU.add)
+                                    in1=b2_wide[:, d, :], op=ALU.add)
 
         def quantise_eo(b):
             nc.vector.quantize_mx(out=eo_codes[:, b, :].bitcast(FP8X4), scales=eo_scales[:, b, :],
@@ -242,7 +255,6 @@ def tile_softmoe_pb_t_e_kernel(tc, h, w2_words, w2_scales, b2, logits, out):
         h_by_tile = h.rearrange("b e s k -> (b e s) k").rearrange("(n p) k -> p n k", p=P)
         scale_rows = w2_scales.rearrange("g (qq r) n -> r qq g n", r=4)
         w2_words_by_p = w2_words.rearrange("g p n t -> p g (n t)").bitcast(I32)
-        b2_by_q = b2.rearrange("(t q) d -> q t d", q=Q)
 
         def load_h(first, last):
             nc.sync.dma_start(out=h_rows[:, T * first:T * last, :], in_=h_by_tile[:, T * first:T * last, :])
@@ -264,8 +276,6 @@ def tile_softmoe_pb_t_e_kernel(tc, h, w2_words, w2_scales, b2, logits, out):
         load_w2(2)
         load_w2(3)
         load(5)
-        for q in range(Q):
-            nc.sync.dma_start(out=b2_rows[S * q:S * q + S, :, :], in_=b2_by_q[q].partition_broadcast(S))
         load_h(2, 4)
 
         TURN = {0: 0, 1: 1, 3: 2, 5: 3}
@@ -276,6 +286,8 @@ def tile_softmoe_pb_t_e_kernel(tc, h, w2_words, w2_scales, b2, logits, out):
             for c in range(D_CHUNKS):
                 MULTIPLY[4 * b - 2 + c] = [(b, c, t) for t in range(T)]
 
+        widen_b2()
+        nc.vector.memset(padded[0][:].bitcast(I32), 0)
         added = -1
         made = -1
         combined = 0

@@ -26,7 +26,7 @@ PITCH = T * P + S
 FIRST_STEP = -2
 EO_STEP = 2
 LAST_STEP = GROUPS + 1
-LAG = 4
+LAG = 3
 
 FLOPS = 2 * B * E * S * H * D + 2 * B * L * K * D
 
@@ -67,7 +67,8 @@ def tile_softmoe_pb_t_e_kernel(tc, h, w2_words, w2_scales, b2, logits, out):
         nc.vector.memset(b2_rows[:], 0.0)
         padded = [const.tile([P, Q * PITCH], U32, align_bytes=64, name="padded%d" % i) for i in range(2)]
         nc.sync.dma_start(out=b2_rows[0:E, :], in_=b2)
-        nc.vector.memset(w2_planes[:].bitcast(I32), 0)
+        for tile in (w2_planes, padded[0], padded[1]):
+            nc.gpsimd.memset(tile[:].bitcast(I32), 0)
 
         x_of, folded, neg_max_of, ex_of, ex_sum_of, inv_sum_of = {}, {}, {}, {}, {}, {}
         cw_of, banks_of, cw_t_of, codes_of, scales_of = {}, {}, {}, {}, {}
@@ -191,8 +192,8 @@ def tile_softmoe_pb_t_e_kernel(tc, h, w2_words, w2_scales, b2, logits, out):
                                   in_=h_codes_of[b][:].rearrange("p (t q s) -> p q t s", t=T, q=Q).bitcast(I32))
 
         def widen_b2():
-            nc.vector.tensor_copy(out=pick[:].rearrange("p t (q s) -> p (t q) s", s=S),
-                                  in_=ident_f32[:, 0:E].unsqueeze(2).to_broadcast([P, E, S]))
+            nc.scalar.copy(out=pick[:].rearrange("p t (q s) -> p (t q) s", s=S),
+                           in_=ident_f32[:, 0:E].unsqueeze(2).to_broadcast([P, E, S]))
             for c in range(D_CHUNKS):
                 bank = psum_mm.tile([P, T, P], F32, tag="bank_mm")
                 for t in range(T):
@@ -287,7 +288,6 @@ def tile_softmoe_pb_t_e_kernel(tc, h, w2_words, w2_scales, b2, logits, out):
                 MULTIPLY[4 * b - 2 + c] = [(b, c, t) for t in range(T)]
 
         widen_b2()
-        nc.vector.memset(padded[0][:].bitcast(I32), 0)
         added = -1
         made = -1
         combined = 0
@@ -308,12 +308,12 @@ def tile_softmoe_pb_t_e_kernel(tc, h, w2_words, w2_scales, b2, logits, out):
             invert_sum(s)
             normalise(s, range(2, J), nc.gpsimd)
             transposes(s - 1)
-            top = s - LAG if s < GROUPS - 1 else s - 2 if draining else s - 3
+            top = s - 2 if draining else s - LAG
             ready = [g for g in range(combined, GROUPS) if g <= top and g // GROUPS_PER_BATCH <= made][:2]
             combined += len(ready)
             for g in ready:
                 combine(g)
-            exps(s + 1, range(0, 2))
+            exps(s + 1, range(0, 4 if s == 3 else 2))
             copy_out(s - 1, 0, False)
             for b, c in pending:
                 add_b2(b, c)
@@ -321,7 +321,7 @@ def tile_softmoe_pb_t_e_kernel(tc, h, w2_words, w2_scales, b2, logits, out):
                     added = b
             pending = []
             finish_max(s + 2)
-            copy_out(s - 1, 1, len(ready) == 0)
+            copy_out(s - 1, 1, len(ready) == 0 or s % 2 == 0)
             normalise(s, range(0, 2), nc.vector)
             for i, g in enumerate(ready):
                 for half in range(2):
@@ -329,7 +329,7 @@ def tile_softmoe_pb_t_e_kernel(tc, h, w2_words, w2_scales, b2, logits, out):
                         on_vector = s >= GROUPS - 1 and j % 2 == 1
                         take_out(g, j, nc.vector.tensor_copy if on_vector else nc.scalar.copy)
                     store(g, half)
-                    if i == 0 and half == 0:
+                    if i == 0 and half == 0 and s != 3:
                         exps(s + 1, range(2, 4))
             if not ready:
                 exps(s + 1, range(2, 4))
@@ -341,6 +341,9 @@ def tile_softmoe_pb_t_e_kernel(tc, h, w2_words, w2_scales, b2, logits, out):
                 multiply_eo(b, c, t)
                 if t == T - 1:
                     pending.append((b, c))
-            if s == -1:
-                nc.vector.memset(padded[1][:].bitcast(I32), 0)
+            if s == 2:
+                for b, c in pending:
+                    add_b2(b, c)
+                pending = []
+                added = 0
         assert combined == GROUPS

@@ -67,8 +67,8 @@ def tile_softmoe_pb_t_e_kernel(tc, h, w2_words, w2_scales, b2, logits, out):
         nc.vector.memset(b2_rows[:], 0.0)
         padded = [const.tile([P, Q * PITCH], U32, align_bytes=64, name="padded%d" % i) for i in range(2)]
         nc.sync.dma_start(out=b2_rows[0:E, :], in_=b2)
-        for tile in (w2_planes, padded[0], padded[1]):
-            nc.gpsimd.memset(tile[:].bitcast(I32), 0)
+        for tile in (w2_planes, padded[0]):
+            nc.vector.memset(tile[:].bitcast(I32), 0)
 
         x_of, folded, neg_max_of, ex_of, ex_sum_of, inv_sum_of = {}, {}, {}, {}, {}, {}
         cw_of, banks_of, cw_t_of, codes_of, scales_of = {}, {}, {}, {}, {}
@@ -76,31 +76,35 @@ def tile_softmoe_pb_t_e_kernel(tc, h, w2_words, w2_scales, b2, logits, out):
         def is_group(g):
             return 0 <= g < GROUPS
 
-        def load(g):
+        def load(g, pieces=1):
             if not is_group(g) or g in x_of:
                 return
-            rows = logits_rows[g * P * J:(g + 1) * P * J, :]
+            rows = logits_rows[g * P * J:(g + 1) * P * J, :].rearrange("(p j) k -> p j k", j=J)
             x = xs.tile([P, J, K], BF16)
-            nc.sync.dma_start(out=x[:], in_=rows.rearrange("(p j) k -> p j k", j=J))
+            for i in range(pieces):
+                tiles = slice(i * J // pieces, (i + 1) * J // pieces)
+                nc.sync.dma_start(out=x[:, tiles, :], in_=rows[:, tiles, :])
             x_of[g] = x
 
-        def fold_max(g, level):
+        def fold_max(g, level, tiles=slice(0, J)):
             if not is_group(g):
                 return
             wide = x_of[g] if level == 0 else folded[(g, level - 1)]
             width = K >> (level + 1)
-            half = stage.tile([P, J, width], BF16, name="fold%d" % level)
-            nc.vector.tensor_tensor(out=half[:], in0=wide[:, :, 0:width], in1=wide[:, :, width:2 * width],
-                                    op=ALU.max)
-            folded[(g, level)] = half
+            if (g, level) not in folded:
+                half = stage.tile([P, J, width], BF16, name="fold%d" % level)
+                folded[(g, level)] = half
+            nc.vector.tensor_tensor(out=folded[(g, level)][:, tiles, :], in0=wide[:, tiles, 0:width],
+                                    in1=wide[:, tiles, width:2 * width], op=ALU.max)
 
-        def finish_max(g):
+        def finish_max(g, tiles=slice(0, J)):
             if not is_group(g):
                 return
-            neg_max = small.tile([P, J], F32)
-            nc.vector.tensor_reduce(out=neg_max[:], in_=folded[(g, FOLDS - 1)][:],
+            if g not in neg_max_of:
+                neg_max = small.tile([P, J], F32)
+                neg_max_of[g] = neg_max
+            nc.vector.tensor_reduce(out=neg_max_of[g][:, tiles], in_=folded[(g, FOLDS - 1)][:, tiles, :],
                                     axis=mybir.AxisListType.X, op=ALU.max, negate=True)
-            neg_max_of[g] = neg_max
 
         def exps(g, tiles):
             if not is_group(g):
@@ -231,6 +235,16 @@ def tile_softmoe_pb_t_e_kernel(tc, h, w2_words, w2_scales, b2, logits, out):
 
         acc_of, o_of = {}, {}
 
+        def keep_warm(g, passes):
+            fill = psum_e.tile([P, D], F32, tag="bank_e")
+            for i in range(passes):
+                nc.tensor.matmul_mx(out=fill[:],
+                                    lhsT=codes_of[g][:, 0:P].bitcast(FP8X4),
+                                    lhsT_scale=scales_of[g][:, 0:P],
+                                    rhs=eo_codes[:, g // GROUPS_PER_BATCH, :].bitcast(FP8X4),
+                                    rhs_scale=eo_scales[:, g // GROUPS_PER_BATCH, :],
+                                    start=True, stop=True)
+
         def combine(g):
             b = g // GROUPS_PER_BATCH
             for j in range(J):
@@ -264,7 +278,7 @@ def tile_softmoe_pb_t_e_kernel(tc, h, w2_words, w2_scales, b2, logits, out):
             nc.sync.dma_start(out=w2_codes[:, Q * t:Q * t + Q, :].bitcast(I32),
                               in_=w2_words_by_p[:, Q * t:Q * t + Q, :])
 
-        load(0)
+        load(0, 1)
         load(1)
         load_h(0, 2)
         load(2)
@@ -299,40 +313,55 @@ def tile_softmoe_pb_t_e_kernel(tc, h, w2_words, w2_scales, b2, logits, out):
             if added > made:
                 quantise_eo(added)
                 made = added
-            fold_max(s + 2, 0)
-            quantise(s - 2)
-            fold_max(s + 2, 1)
+            if s == FIRST_STEP:
+                for i in range(1):
+                    tiles = slice(i * J // 1, (i + 1) * J // 1)
+                    for level in range(FOLDS):
+                        fold_max(0, level, tiles)
+                    finish_max(0, tiles)
+            else:
+                fold_max(s + 2, 0)
+                quantise(s - 2)
+                fold_max(s + 2, 1)
             if s - 1 in TURN:
                 quantise_h(TURN[s - 1])
                 spread(TURN[s - 1])
             invert_sum(s)
-            normalise(s, range(2, J), nc.gpsimd)
+            normalise(s, range((4 if s == 0 else 2), J), nc.gpsimd)
             transposes(s - 1)
-            top = s - 2 if draining else s - LAG
+            top = s - 2 if draining else s - 3 if s == GROUPS - 1 else s - LAG
             ready = [g for g in range(combined, GROUPS) if g <= top and g // GROUPS_PER_BATCH <= made][:2]
             combined += len(ready)
             for g in ready:
                 combine(g)
-            exps(s + 1, range(0, 4 if s == 3 else 2))
+            if ready and 0:
+                keep_warm(ready[-1], 0)
+            exps(s + 1, range(0, 4 if s == 3 and True else 2))
             copy_out(s - 1, 0, False)
             for b, c in pending:
                 add_b2(b, c)
                 if c == D_CHUNKS - 1:
                     added = b
             pending = []
-            finish_max(s + 2)
+            if s > FIRST_STEP:
+                finish_max(s + 2)
             copy_out(s - 1, 1, len(ready) == 0 or s % 2 == 0)
-            normalise(s, range(0, 2), nc.vector)
+            normalise(s, range(0, (4 if s == 0 else 2)), nc.vector)
             for i, g in enumerate(ready):
                 for half in range(2):
                     for j in (2 * half, 2 * half + 1):
                         on_vector = s >= GROUPS - 1 and j % 2 == 1
                         take_out(g, j, nc.vector.tensor_copy if on_vector else nc.scalar.copy)
-                    store(g, half)
-                    if i == 0 and half == 0 and s != 3:
+                        if g == GROUPS - 1 and False:
+                            nc.sync.dma_start(out=out_rows[g * P * J:(g + 1) * P * J, :].rearrange("(p j) d -> p j d", j=J)[:, j:j + 1, :], in_=o_of[(g, half)][:, j % 2:j % 2 + 1, :])
+                    if not (g == GROUPS - 1 and False):
+                        store(g, half)
+                    if i == 0 and half == 0 and not (s == 3 and True):
                         exps(s + 1, range(2, 4))
             if not ready:
                 exps(s + 1, range(2, 4))
+            if s == -1:
+                nc.vector.memset(padded[1][:].bitcast(I32), 0)
             if s in TURN:
                 turn_h(TURN[s])
             for b, c, t in MULTIPLY.get(s, []):
@@ -341,7 +370,7 @@ def tile_softmoe_pb_t_e_kernel(tc, h, w2_words, w2_scales, b2, logits, out):
                 multiply_eo(b, c, t)
                 if t == T - 1:
                     pending.append((b, c))
-            if s == 2:
+            if s == 2 and True:
                 for b, c in pending:
                     add_b2(b, c)
                 pending = []

@@ -66,7 +66,6 @@ def tile_softmoe_pb_t_e_kernel(tc, h, w2_words, w2_scales, b2, logits, out):
         b2_wide = const.tile([P, D, T], BF16)
         nc.vector.memset(b2_rows[:], 0.0)
         padded = [const.tile([P, Q * PITCH], U32, align_bytes=64, name="padded%d" % i) for i in range(2)]
-        nc.sync.dma_start(out=b2_rows[0:E, :], in_=b2)
         for tile in (w2_planes, padded[0]):
             nc.vector.memset(tile[:].bitcast(I32), 0)
 
@@ -106,6 +105,15 @@ def tile_softmoe_pb_t_e_kernel(tc, h, w2_words, w2_scales, b2, logits, out):
             nc.vector.tensor_reduce(out=neg_max_of[g][:, tiles], in_=folded[(g, FOLDS - 1)][:, tiles, :],
                                     axis=mybir.AxisListType.X, op=ALU.max, negate=True)
 
+        def EXS(g, j):
+            return j < 2
+
+        def pairs_apart(row):
+            return row.rearrange("p (u e q) -> p u q e", u=2, e=2)
+
+        def pairs_together(row):
+            return row.rearrange("p (u q e) -> p u q e", u=2, e=2)
+
         def exps(g, tiles):
             if not is_group(g):
                 return
@@ -114,8 +122,10 @@ def tile_softmoe_pb_t_e_kernel(tc, h, w2_words, w2_scales, b2, logits, out):
                 ex_sum = small.tile([P, J], F32)
                 ex_of[g], ex_sum_of[g] = ex, ex_sum
             for j in tiles:
-                nc.scalar.activation(out=ex_of[g][:, j, :].rearrange("p (u q e) -> p u q e", u=2, e=2),
-                                     in_=x_of[g][:, j, :].rearrange("p (u e q) -> p u q e", u=2, e=2),
+                row, ex = x_of[g][:, j, :], ex_of[g][:, j, :]
+                if EXS(g, j):
+                    row, ex = pairs_apart(row), pairs_together(ex)
+                nc.scalar.activation(out=ex, in_=row,
                                      func=ACT.Exp,
                                      bias=neg_max_of[g][:, j:j + 1], scale=1.0,
                                      accum_out=ex_sum_of[g][:, j:j + 1])
@@ -134,14 +144,17 @@ def tile_softmoe_pb_t_e_kernel(tc, h, w2_words, w2_scales, b2, logits, out):
                 cw = work.tile([P, J, K], BF16)
                 cw_of[g] = cw
             for j in tiles:
-                engine.tensor_scalar(out=cw_of[g][:, j, :], in0=ex_of[g][:, j, :],
+                ex, cw = ex_of[g][:, j, :], cw_of[g][:, j, :]
+                if not EXS(g, j):
+                    ex, cw = pairs_apart(ex), pairs_together(cw)
+                engine.tensor_scalar(out=cw, in0=ex,
                                      scalar1=inv_sum_of[g][:, j:j + 1], scalar2=0.0,
                                      op0=ALU.mult, op1=ALU.add)
 
-        def transposes(g):
+        def transposes(g, pairs=range(J // 2)):
             if not is_group(g):
                 return
-            for pair in range(J // 2):
+            for pair in pairs:
                 bank = psum_t.tile([P, 2, 2, P], F32, tag="bank_t")
                 for i in range(2):
                     words = cw_of[g][:, 2 * pair + i, :].bitcast(F32)
@@ -159,14 +172,16 @@ def tile_softmoe_pb_t_e_kernel(tc, h, w2_words, w2_scales, b2, logits, out):
             copy(out=cw_t_of[g][:].bitcast(F32)[:, 2 * pair:2 * pair + 2, :, :],
                  in_=banks_of[(g, pair)][:].rearrange("q u i l -> q i l u"))
 
-        def quantise(g):
+        def quantise(g, tiles=slice(0, J)):
             if not is_group(g):
                 return
-            codes = cwq.tile([P, J * P], U32, align_bytes=64)
-            scales = cwq.tile([P, J * P], U8, align_bytes=64)
-            nc.vector.quantize_mx(out=codes[:].bitcast(FP8X4), scales=scales[:],
-                                  in_=cw_t_of[g][:].rearrange("q j l t -> q (j l t)"))
-            codes_of[g], scales_of[g] = codes, scales
+            if g not in codes_of:
+                codes = cwq.tile([P, J, P], U32, align_bytes=64)
+                scales = cwq.tile([P, J, P], U8, align_bytes=64)
+                codes_of[g], scales_of[g] = codes, scales
+            nc.vector.quantize_mx(out=codes_of[g][:, tiles, :].rearrange("q j l -> q (j l)").bitcast(FP8X4),
+                                  scales=scales_of[g][:, tiles, :].rearrange("q j l -> q (j l)"),
+                                  in_=cw_t_of[g][:, tiles, :, :].rearrange("q j l t -> q (j l t)"))
 
         h_t_of, h_codes_of, eo_banks, eo_k_of = {}, {}, {}, {}
 
@@ -235,23 +250,13 @@ def tile_softmoe_pb_t_e_kernel(tc, h, w2_words, w2_scales, b2, logits, out):
 
         acc_of, o_of = {}, {}
 
-        def keep_warm(g, passes):
-            fill = psum_e.tile([P, D], F32, tag="bank_e")
-            for i in range(passes):
-                nc.tensor.matmul_mx(out=fill[:],
-                                    lhsT=codes_of[g][:, 0:P].bitcast(FP8X4),
-                                    lhsT_scale=scales_of[g][:, 0:P],
-                                    rhs=eo_codes[:, g // GROUPS_PER_BATCH, :].bitcast(FP8X4),
-                                    rhs_scale=eo_scales[:, g // GROUPS_PER_BATCH, :],
-                                    start=True, stop=True)
-
-        def combine(g):
+        def combine(g, tiles=range(J)):
             b = g // GROUPS_PER_BATCH
-            for j in range(J):
+            for j in tiles:
                 acc = psum_mm.tile([P, D], F32, tag="bank_mm")
                 nc.tensor.matmul_mx(out=acc[:],
-                                    lhsT=codes_of[g][:, j * P:(j + 1) * P].bitcast(FP8X4),
-                                    lhsT_scale=scales_of[g][:, j * P:(j + 1) * P],
+                                    lhsT=codes_of[g][:, j, :].bitcast(FP8X4),
+                                    lhsT_scale=scales_of[g][:, j, :],
                                     rhs=eo_codes[:, b, :].bitcast(FP8X4),
                                     rhs_scale=eo_scales[:, b, :],
                                     start=True, stop=True)
@@ -279,6 +284,7 @@ def tile_softmoe_pb_t_e_kernel(tc, h, w2_words, w2_scales, b2, logits, out):
                               in_=w2_words_by_p[:, Q * t:Q * t + Q, :])
 
         load(0, 1)
+        nc.sync.dma_start(out=b2_rows[0:E, :], in_=b2)
         load(1)
         load_h(0, 2)
         load(2)
@@ -299,14 +305,14 @@ def tile_softmoe_pb_t_e_kernel(tc, h, w2_words, w2_scales, b2, logits, out):
                     3: [(1, 0, t) for t in range(T)], 4: [(1, c, t) for c in (1, 2) for t in range(T)], 5: [(1, 3, t) for t in range(T)]}
         for b in range(2, B):
             for c in range(D_CHUNKS):
-                MULTIPLY[4 * b - 2 + c] = [(b, c, t) for t in range(T)]
+                MULTIPLY.setdefault(4 * b - 2 + c - b // 3, []).extend([(b, c, t) for t in range(T)])
 
         widen_b2()
         added = -1
         made = -1
         combined = 0
         pending = []
-        for s in range(FIRST_STEP, LAST_STEP + 1):
+        for s in range(FIRST_STEP, GROUPS - 1):
             draining = s >= GROUPS
             load(s + LOAD_AHEAD)
 
@@ -329,14 +335,12 @@ def tile_softmoe_pb_t_e_kernel(tc, h, w2_words, w2_scales, b2, logits, out):
             invert_sum(s)
             normalise(s, range((4 if s == 0 else 2), J), nc.gpsimd)
             transposes(s - 1)
-            top = s - 2 if draining else s - 3 if s == GROUPS - 1 else s - LAG
+            top = s - 2 if draining else s - LAG
             ready = [g for g in range(combined, GROUPS) if g <= top and g // GROUPS_PER_BATCH <= made][:2]
             combined += len(ready)
             for g in ready:
                 combine(g)
-            if ready and 0:
-                keep_warm(ready[-1], 0)
-            exps(s + 1, range(0, 4 if s == 3 and True else 2))
+            exps(s + 1, range(0, (4 if s == 3 else 2)))
             copy_out(s - 1, 0, False)
             for b, c in pending:
                 add_b2(b, c)
@@ -345,7 +349,7 @@ def tile_softmoe_pb_t_e_kernel(tc, h, w2_words, w2_scales, b2, logits, out):
             pending = []
             if s > FIRST_STEP:
                 finish_max(s + 2)
-            copy_out(s - 1, 1, len(ready) == 0 or s % 2 == 0)
+            copy_out(s - 1, 1, len(ready) == 0 or s % 4 == 0)
             normalise(s, range(0, (4 if s == 0 else 2)), nc.vector)
             for i, g in enumerate(ready):
                 for half in range(2):
@@ -356,10 +360,10 @@ def tile_softmoe_pb_t_e_kernel(tc, h, w2_words, w2_scales, b2, logits, out):
                             nc.sync.dma_start(out=out_rows[g * P * J:(g + 1) * P * J, :].rearrange("(p j) d -> p j d", j=J)[:, j:j + 1, :], in_=o_of[(g, half)][:, j % 2:j % 2 + 1, :])
                     if not (g == GROUPS - 1 and False):
                         store(g, half)
-                    if i == 0 and half == 0 and not (s == 3 and True):
-                        exps(s + 1, range(2, 4))
+                    if i == 0 and half == 0:
+                        exps(s + 1, range((4 if s == 3 else 2), 4))
             if not ready:
-                exps(s + 1, range(2, 4))
+                exps(s + 1, range((4 if s == 3 else 2), 4))
             if s == -1:
                 nc.vector.memset(padded[1][:].bitcast(I32), 0)
             if s in TURN:
@@ -375,4 +379,38 @@ def tile_softmoe_pb_t_e_kernel(tc, h, w2_words, w2_scales, b2, logits, out):
                     add_b2(b, c)
                 pending = []
                 added = 0
-        assert combined == GROUPS
+        last = GROUPS - 1
+        first = combined
+        assert first == last - 3 and added == B - 1
+
+        def results(g, tiles, copies):
+            for j, copy in zip(tiles, copies):
+                take_out(g, j, copy)
+                if j % 2 == 1:
+                    store(g, j // 2)
+
+        if made < added:
+            quantise_eo(added)
+        on_scalar, on_vector = nc.scalar.copy, nc.vector.tensor_copy
+        transposes(last - 1)
+        combine(last - 3)
+        quantise(last - 2)
+        copy_out(last - 1, 0, False)
+        copy_out(last - 1, 1, False)
+        invert_sum(last)
+        results(last - 3, range(J), [on_scalar] * J)
+        combine(last - 2, range(0, 2))
+        normalise(last, range(0, 2), nc.vector)
+        transposes(last, range(0, 1))
+        normalise(last, range(2, J), nc.vector)
+        combine(last - 2, range(2, J))
+        results(last - 2, range(J), [on_scalar] * J)
+        transposes(last, range(1, 2))
+        quantise(last - 1)
+        copy_out(last, 0, False)
+        copy_out(last, 1, False)
+        combine(last - 1)
+        quantise(last)
+        results(last - 1, range(J), [on_scalar, on_scalar, on_vector, on_vector])
+        combine(last)
+        results(last, range(J), [on_scalar, on_vector, on_scalar, on_vector])

@@ -106,7 +106,7 @@ def tile_softmoe_pb_t_e_kernel(tc, h, w2_words, w2_scales, b2, logits, out):
                                     axis=mybir.AxisListType.X, op=ALU.max, negate=True)
 
         def EXS(g, j):
-            return j < 2
+            return 0 < g < GROUPS - 1 and j >= 2
 
         def pairs_apart(row):
             return row.rearrange("p (u e q) -> p u q e", u=2, e=2)
@@ -349,7 +349,7 @@ def tile_softmoe_pb_t_e_kernel(tc, h, w2_words, w2_scales, b2, logits, out):
             pending = []
             if s > FIRST_STEP:
                 finish_max(s + 2)
-            copy_out(s - 1, 1, len(ready) == 0 or s % 4 == 0)
+            copy_out(s - 1, 1, len(ready) == 0)
             normalise(s, range(0, (4 if s == 0 else 2)), nc.vector)
             for i, g in enumerate(ready):
                 for half in range(2):

@@ -44,7 +44,7 @@ def tile_softmoe_pb_t_e_kernel(tc, h, w2_words, w2_scales, b2, logits, out):
             tc.tile_pool(name="work", bufs=3) as work, \
             tc.tile_pool(name="stage", bufs=2) as stage, \
             tc.tile_pool(name="cwq", bufs=8) as cwq, \
-            tc.tile_pool(name="outs", bufs=6) as outs, \
+            tc.tile_pool(name="outs", bufs=8) as outs, \
             tc.psum_pool(name="psum_t", bufs=2) as psum_t, \
             tc.psum_pool(name="psum_e", bufs=2) as psum_e, \
             tc.psum_pool(name="psum_mm", bufs=4) as psum_mm:
@@ -65,9 +65,9 @@ def tile_softmoe_pb_t_e_kernel(tc, h, w2_words, w2_scales, b2, logits, out):
         pick = const.tile([P, T, P], BF16)
         b2_wide = const.tile([P, D, T], BF16)
         nc.vector.memset(b2_rows[:], 0.0)
-        padded = [const.tile([P, Q * PITCH], U32, align_bytes=64, name="padded%d" % i) for i in range(2)]
-        for tile in (w2_planes, padded[0]):
-            nc.vector.memset(tile[:].bitcast(I32), 0)
+        padded = const.tile([P, Q * PITCH], U32, align_bytes=64)
+        nc.vector.memset(w2_planes[:].bitcast(I32), 0)
+        nc.vector.memset(padded[:].bitcast(I32), 0)
 
         x_of, folded, neg_max_of, ex_of, ex_sum_of, inv_sum_of = {}, {}, {}, {}, {}, {}
         cw_of, banks_of, cw_t_of, codes_of, scales_of = {}, {}, {}, {}, {}
@@ -189,7 +189,8 @@ def tile_softmoe_pb_t_e_kernel(tc, h, w2_words, w2_scales, b2, logits, out):
             h_t = stage.tile([P, T * P, 4], BF16, align_bytes=64)
             h_t_words = h_t[:].bitcast(F32).rearrange("p (t m) u -> p t m u", m=P)
             for half in range(2):
-                bank = psum_mm.tile([P, 2, 2, P], F32, tag="bank_mm")
+                pool, tag = (psum_e, "bank_e") if b < 2 else (psum_mm, "bank_mm")
+                bank = pool.tile([P, 2, 2, P], F32, tag=tag)
                 for i in range(2):
                     words = h_rows[:, T * b + 2 * half + i, :].bitcast(F32)
                     for u in range(2):
@@ -205,15 +206,16 @@ def tile_softmoe_pb_t_e_kernel(tc, h, w2_words, w2_scales, b2, logits, out):
             h_codes_of[b] = h_codes
 
         def spread(b):
-            own = padded[b % 2][:].rearrange("p (q w) -> p q w", q=Q)[:, :, 0:T * P]
+            own = padded[:].rearrange("p (q w) -> p q w", q=Q)[:, :, 0:T * P]
             own = own.rearrange("p q (t m) -> p q t m", m=P)[:, :, :, 0:S]
             nc.vector.tensor_copy(out=own.bitcast(I32),
                                   in_=h_codes_of[b][:].rearrange("p (t q s) -> p q t s", t=T, q=Q).bitcast(I32))
 
-        def widen_b2():
-            nc.scalar.copy(out=pick[:].rearrange("p t (q s) -> p (t q) s", s=S),
+        def widen_b2(chunks):
+            if chunks[0] == 0:
+              nc.scalar.copy(out=pick[:].rearrange("p t (q s) -> p (t q) s", s=S),
                            in_=ident_f32[:, 0:E].unsqueeze(2).to_broadcast([P, E, S]))
-            for c in range(D_CHUNKS):
+            for c in chunks:
                 bank = psum_mm.tile([P, T, P], F32, tag="bank_mm")
                 for t in range(T):
                     nc.tensor.matmul(bank[:, t, :], lhsT=pick[:, t, :], rhs=b2_rows[:, c * P:(c + 1) * P],
@@ -229,7 +231,7 @@ def tile_softmoe_pb_t_e_kernel(tc, h, w2_words, w2_scales, b2, logits, out):
             for q in range(Q):
                 at = q * T * P + t * P
                 nc.tensor.matmul_mx(out=eo_banks[(b, c)][:, t, :],
-                                    lhsT=padded[b % 2][:, at:at + P].bitcast(FP8X4),
+                                    lhsT=padded[:, at:at + P].bitcast(FP8X4),
                                     lhsT_scale=h_scales[:, b, t * P:(t + 1) * P],
                                     rhs=w2_codes[:, Q * t + q, c * P:(c + 1) * P].bitcast(FP8X4),
                                     rhs_scale=w2_planes[:, Q * t + q, c * P:(c + 1) * P],
@@ -268,6 +270,10 @@ def tile_softmoe_pb_t_e_kernel(tc, h, w2_words, w2_scales, b2, logits, out):
                 o_of[(g, j // 2)] = o
             copy(out=o_of[(g, j // 2)][:, j % 2, :], in_=acc_of[(g, j)][:])
 
+        def store_tile(g, j):
+            rows = out_rows[g * P * J:(g + 1) * P * J, :].rearrange("(p j) d -> p j d", j=J)
+            nc.sync.dma_start(out=rows[:, j:j + 1, :], in_=o_of[(g, j // 2)][:, j % 2:j % 2 + 1, :])
+
         def store(g, half):
             rows = out_rows[g * P * J:(g + 1) * P * J, :].rearrange("(p j) d -> p j d", j=J)
             nc.sync.dma_start(out=rows[:, 2 * half:2 * half + 2, :], in_=o_of[(g, half)][:])
@@ -283,7 +289,7 @@ def tile_softmoe_pb_t_e_kernel(tc, h, w2_words, w2_scales, b2, logits, out):
             nc.sync.dma_start(out=w2_codes[:, Q * t:Q * t + Q, :].bitcast(I32),
                               in_=w2_words_by_p[:, Q * t:Q * t + Q, :])
 
-        load(0, 1)
+        load(0)
         nc.sync.dma_start(out=b2_rows[0:E, :], in_=b2)
         load(1)
         load_h(0, 2)
@@ -300,14 +306,14 @@ def tile_softmoe_pb_t_e_kernel(tc, h, w2_words, w2_scales, b2, logits, out):
         load_h(2, 4)
 
         TURN = {0: 0, 1: 1, 3: 2, 5: 3}
-        MULTIPLY = {1: [(0, c, t) for t in (0, 1) for c in range(D_CHUNKS)],
-                    2: [(0, c, t) for t in (2, 3) for c in range(D_CHUNKS)],
+        SPREAD = {1: 0, 3: 1, 6: 2, 10: 3}
+        MULTIPLY = {1: [(0, c, t) for t in (0,) for c in range(D_CHUNKS)],
+                    2: [(0, c, t) for t in (1, 2, 3) for c in range(D_CHUNKS)],
                     3: [(1, 0, t) for t in range(T)], 4: [(1, c, t) for c in (1, 2) for t in range(T)], 5: [(1, 3, t) for t in range(T)]}
         for b in range(2, B):
             for c in range(D_CHUNKS):
-                MULTIPLY.setdefault(4 * b - 2 + c - b // 3, []).extend([(b, c, t) for t in range(T)])
+                MULTIPLY.setdefault(4 * b - 2 + c - (b == 3 and c > 0), []).extend([(b, c, t) for t in range(T)])
 
-        widen_b2()
         added = -1
         made = -1
         combined = 0
@@ -331,7 +337,8 @@ def tile_softmoe_pb_t_e_kernel(tc, h, w2_words, w2_scales, b2, logits, out):
                 fold_max(s + 2, 1)
             if s - 1 in TURN:
                 quantise_h(TURN[s - 1])
-                spread(TURN[s - 1])
+            if s in SPREAD:
+                spread(SPREAD[s])
             invert_sum(s)
             normalise(s, range((4 if s == 0 else 2), J), nc.gpsimd)
             transposes(s - 1)
@@ -340,7 +347,13 @@ def tile_softmoe_pb_t_e_kernel(tc, h, w2_words, w2_scales, b2, logits, out):
             combined += len(ready)
             for g in ready:
                 combine(g)
-            exps(s + 1, range(0, (4 if s == 3 else 2)))
+            if s == -1 and [0, 1]:
+                widen_b2([0, 1])
+            exps(s + 1, range(0, (4 if s == 3 else 3)))
+            if s == -1 and []:
+                widen_b2([])
+            if s == 0 and []:
+                widen_b2([])
             copy_out(s - 1, 0, False)
             for b, c in pending:
                 add_b2(b, c)
@@ -361,13 +374,15 @@ def tile_softmoe_pb_t_e_kernel(tc, h, w2_words, w2_scales, b2, logits, out):
                     if not (g == GROUPS - 1 and False):
                         store(g, half)
                     if i == 0 and half == 0:
-                        exps(s + 1, range((4 if s == 3 else 2), 4))
+                        exps(s + 1, range((4 if s == 3 else 3), 4))
             if not ready:
-                exps(s + 1, range((4 if s == 3 else 2), 4))
-            if s == -1:
-                nc.vector.memset(padded[1][:].bitcast(I32), 0)
+                exps(s + 1, range((4 if s == 3 else 3), 4))
+            if s == -1 and []:
+                widen_b2([])
             if s in TURN:
                 turn_h(TURN[s])
+            if s == 0 and [2, 3]:
+                widen_b2([2, 3])
             for b, c, t in MULTIPLY.get(s, []):
                 if t == 0:
                     open_eo(b, c)
@@ -386,7 +401,9 @@ def tile_softmoe_pb_t_e_kernel(tc, h, w2_words, w2_scales, b2, logits, out):
         def results(g, tiles, copies):
             for j, copy in zip(tiles, copies):
                 take_out(g, j, copy)
-                if j % 2 == 1:
+                if g == last:
+                    store_tile(g, j)
+                elif j % 2 == 1:
                     store(g, j // 2)
 
         if made < added:
@@ -411,6 +428,6 @@ def tile_softmoe_pb_t_e_kernel(tc, h, w2_words, w2_scales, b2, logits, out):
         copy_out(last, 1, False)
         combine(last - 1)
         quantise(last)
-        results(last - 1, range(J), [on_scalar, on_scalar, on_vector, on_vector])
+        results(last - 1, range(J), [on_scalar, on_scalar, on_scalar, on_vector])
         combine(last)
         results(last, range(J), [on_scalar, on_vector, on_scalar, on_vector])

from concourse import mybir
from concourse.masks import make_identity

F32 = mybir.dt.float32
BF16 = mybir.dt.bfloat16
I32 = mybir.dt.int32
U32 = mybir.dt.uint32
U8 = mybir.dt.uint8
FP8X4 = mybir.dt.float8_e4m3fn_x4
ALU = mybir.AluOpType
ACT = mybir.ActivationFunctionType

P = 128
B, L, D, E, S, H = 4, 2048, 512, 16, 32, 512
K = E * S
J = 4
GROUPS = B * L // (P * J)
GROUPS_PER_BATCH = GROUPS // B
D_CHUNKS = D // P
T = 4
Q = E // T
FOLDS = 2
LOAD_AHEAD = 4
PITCH = T * P + S

FIRST_STEP = -2
EO_STEP = 2
LAST_STEP = GROUPS + 1
LAG = 3

FLOPS = 2 * B * E * S * H * D + 2 * B * L * K * D


def tile_softmoe_pb_t_e_kernel(tc, h, w2_words, w2_scales, b2, logits, out):
    nc = tc.nc

    logits_rows = logits.rearrange("b l e s -> (b l) (e s)")
    out_rows = out.rearrange("b l d -> (b l) d")

    with tc.manual_schedule(), \
            tc.tile_pool(name="const", bufs=1) as const, \
            tc.tile_pool(name="small", bufs=4) as small, \
            tc.tile_pool(name="xs", bufs=6) as xs, \
            tc.tile_pool(name="work", bufs=3) as work, \
            tc.tile_pool(name="stage", bufs=2) as stage, \
            tc.tile_pool(name="cwq", bufs=8) as cwq, \
            tc.tile_pool(name="outs", bufs=8) as outs, \
            tc.psum_pool(name="psum_t", bufs=2) as psum_t, \
            tc.psum_pool(name="psum_e", bufs=2) as psum_e, \
            tc.psum_pool(name="psum_mm", bufs=4) as psum_mm:

        ident_f32 = const.tile([P, P], F32)
        make_identity(nc, ident_f32[:])
        warm = const.tile([P, 1], F32)
        nc.vector.memset(warm[:], 0.0)
        nc.scalar.activation(out=warm[:], in_=warm[:], func=ACT.Exp)

        eo_codes = const.tile([P, B, D], U32, align_bytes=64)
        eo_scales = const.tile([P, B, D], U8, align_bytes=64)
        w2_planes = const.tile([P, E, D], U8, align_bytes=64)
        w2_codes = const.tile([P, E, D], U32, align_bytes=64)
        h_rows = const.tile([P, B * T, H], BF16)
        h_scales = const.tile([P, B, T * P], U8, align_bytes=64)
        b2_rows = const.tile([P, D], BF16)
        pick = const.tile([P, T, P], BF16)
        b2_wide = const.tile([P, D, T], BF16)
        nc.vector.memset(b2_rows[:], 0.0)
        padded = const.tile([P, Q * PITCH], U32, align_bytes=64)
        nc.vector.memset(w2_planes[:].bitcast(I32), 0)
        nc.vector.memset(padded[:].bitcast(I32), 0)

        x_of, folded, neg_max_of, ex_of, ex_sum_of, inv_sum_of = {}, {}, {}, {}, {}, {}
        cw_of, banks_of, cw_t_of, codes_of, scales_of = {}, {}, {}, {}, {}

        def is_group(g):
            return 0 <= g < GROUPS

        def load(g, pieces=1):
            if not is_group(g) or g in x_of:
                return
            rows = logits_rows[g * P * J:(g + 1) * P * J, :].rearrange("(p j) k -> p j k", j=J)
            x = xs.tile([P, J, K], BF16)
            for i in range(pieces):
                tiles = slice(i * J // pieces, (i + 1) * J // pieces)
                nc.sync.dma_start(out=x[:, tiles, :], in_=rows[:, tiles, :])
            x_of[g] = x

        def fold_max(g, level, tiles=slice(0, J)):
            if not is_group(g):
                return
            wide = x_of[g] if level == 0 else folded[(g, level - 1)]
            width = K >> (level + 1)
            if (g, level) not in folded:
                half = stage.tile([P, J, width], BF16, name="fold%d" % level)
                folded[(g, level)] = half
            nc.vector.tensor_tensor(out=folded[(g, level)][:, tiles, :], in0=wide[:, tiles, 0:width],
                                    in1=wide[:, tiles, width:2 * width], op=ALU.max)

        def finish_max(g, tiles=slice(0, J)):
            if not is_group(g):
                return
            if g not in neg_max_of:
                neg_max = small.tile([P, J], F32)
                neg_max_of[g] = neg_max
            nc.vector.tensor_reduce(out=neg_max_of[g][:, tiles], in_=folded[(g, FOLDS - 1)][:, tiles, :],
                                    axis=mybir.AxisListType.X, op=ALU.max, negate=True)

        def EXS(g, j):
            return 0 < g < GROUPS - 1 and j >= 2

        def pairs_apart(row):
            return row.rearrange("p (u e q) -> p u q e", u=2, e=2)

        def pairs_together(row):
            return row.rearrange("p (u q e) -> p u q e", u=2, e=2)

        def exps(g, tiles):
            if not is_group(g):
                return
            if g not in ex_of:
                ex = work.tile([P, J, K], F32)
                ex_sum = small.tile([P, J], F32)
                ex_of[g], ex_sum_of[g] = ex, ex_sum
            for j in tiles:
                row, ex = x_of[g][:, j, :], ex_of[g][:, j, :]
                if EXS(g, j):
                    row, ex = pairs_apart(row), pairs_together(ex)
                nc.scalar.activation(out=ex, in_=row,
                                     func=ACT.Exp,
                                     bias=neg_max_of[g][:, j:j + 1], scale=1.0,
                                     accum_out=ex_sum_of[g][:, j:j + 1])

        def invert_sum(g):
            if not is_group(g):
                return
            inv_sum = small.tile([P, J], F32)
            nc.vector.reciprocal(out=inv_sum[:], in_=ex_sum_of[g][:])
            inv_sum_of[g] = inv_sum

        def normalise(g, tiles, engine):
            if not is_group(g):
                return
            if g not in cw_of:
                cw = work.tile([P, J, K], BF16)
                cw_of[g] = cw
            for j in tiles:
                ex, cw = ex_of[g][:, j, :], cw_of[g][:, j, :]
                if not EXS(g, j):
                    ex, cw = pairs_apart(ex), pairs_together(cw)
                engine.tensor_scalar(out=cw, in0=ex,
                                     scalar1=inv_sum_of[g][:, j:j + 1], scalar2=0.0,
                                     op0=ALU.mult, op1=ALU.add)

        def transposes(g, pairs=range(J // 2)):
            if not is_group(g):
                return
            for pair in pairs:
                bank = psum_t.tile([P, 2, 2, P], F32, tag="bank_t")
                for i in range(2):
                    words = cw_of[g][:, 2 * pair + i, :].bitcast(F32)
                    for u in range(2):
                        nc.tensor.transpose(bank[:, u, i, :], words[:, u * P:(u + 1) * P], ident_f32[:])
                banks_of[(g, pair)] = bank

        def copy_out(g, pair, on_scalar):
            if not is_group(g):
                return
            if pair == 0:
                cw_t = stage.tile([P, J, P, 4], BF16, align_bytes=64)
                cw_t_of[g] = cw_t
            copy = nc.scalar.copy if on_scalar else nc.vector.tensor_copy
            copy(out=cw_t_of[g][:].bitcast(F32)[:, 2 * pair:2 * pair + 2, :, :],
                 in_=banks_of[(g, pair)][:].rearrange("q u i l -> q i l u"))

        def quantise(g, tiles=slice(0, J)):
            if not is_group(g):
                return
            if g not in codes_of:
                codes = cwq.tile([P, J, P], U32, align_bytes=64)
                scales = cwq.tile([P, J, P], U8, align_bytes=64)
                codes_of[g], scales_of[g] = codes, scales
            nc.vector.quantize_mx(out=codes_of[g][:, tiles, :].rearrange("q j l -> q (j l)").bitcast(FP8X4),
                                  scales=scales_of[g][:, tiles, :].rearrange("q j l -> q (j l)"),
                                  in_=cw_t_of[g][:, tiles, :, :].rearrange("q j l t -> q (j l t)"))

        h_t_of, h_codes_of, eo_banks, eo_k_of = {}, {}, {}, {}

        def turn_h(b):
            h_t = stage.tile([P, T * P, 4], BF16, align_bytes=64)
            h_t_words = h_t[:].bitcast(F32).rearrange("p (t m) u -> p t m u", m=P)
            for half in range(2):
                pool, tag = (psum_e, "bank_e") if b < 2 else (psum_mm, "bank_mm")
                bank = pool.tile([P, 2, 2, P], F32, tag=tag)
                for i in range(2):
                    words = h_rows[:, T * b + 2 * half + i, :].bitcast(F32)
                    for u in range(2):
                        nc.tensor.transpose(bank[:, u, i, :], words[:, u:H // 2:2], ident_f32[:])
                nc.scalar.copy(out=h_t_words[:, 2 * half:2 * half + 2, :, :],
                               in_=bank[:].rearrange("p u i m -> p i m u"))
            h_t_of[b] = h_t

        def quantise_h(b):
            h_codes = stage.tile([P, T * P], U32, align_bytes=64)
            nc.vector.quantize_mx(out=h_codes[:].bitcast(FP8X4), scales=h_scales[:, b, :],
                                  in_=h_t_of[b][:].rearrange("p m t -> p (m t)"))
            h_codes_of[b] = h_codes

        def spread(b):
            own = padded[:].rearrange("p (q w) -> p q w", q=Q)[:, :, 0:T * P]
            own = own.rearrange("p q (t m) -> p q t m", m=P)[:, :, :, 0:S]
            nc.vector.tensor_copy(out=own.bitcast(I32),
                                  in_=h_codes_of[b][:].rearrange("p (t q s) -> p q t s", t=T, q=Q).bitcast(I32))

        def widen_b2(chunks):
            if chunks[0] == 0:
              nc.scalar.copy(out=pick[:].rearrange("p t (q s) -> p (t q) s", s=S),
                           in_=ident_f32[:, 0:E].unsqueeze(2).to_broadcast([P, E, S]))
            for c in chunks:
                bank = psum_mm.tile([P, T, P], F32, tag="bank_mm")
                for t in range(T):
                    nc.tensor.matmul(bank[:, t, :], lhsT=pick[:, t, :], rhs=b2_rows[:, c * P:(c + 1) * P],
                                     start=True, stop=True)
                nc.scalar.copy(out=b2_wide[:, c * P:(c + 1) * P, :], in_=bank[:].rearrange("m t d -> m d t"))

        def open_eo(b, c):
            pool, tag = (psum_mm, "bank_mm") if b == 0 else (psum_e, "bank_e")
            bank = pool.tile([P, T, P], F32, tag=tag)
            eo_banks[(b, c)] = bank

        def multiply_eo(b, c, t):
            for q in range(Q):
                at = q * T * P + t * P
                nc.tensor.matmul_mx(out=eo_banks[(b, c)][:, t, :],
                                    lhsT=padded[:, at:at + P].bitcast(FP8X4),
                                    lhsT_scale=h_scales[:, b, t * P:(t + 1) * P],
                                    rhs=w2_codes[:, Q * t + q, c * P:(c + 1) * P].bitcast(FP8X4),
                                    rhs_scale=w2_planes[:, Q * t + q, c * P:(c + 1) * P],
                                    start=(q == 0), stop=(q == Q - 1))

        def add_b2(b, c):
            if c == 0:
                eo_k = stage.tile([P, D, T], BF16, align_bytes=64)
                eo_k_of[b] = eo_k
            d = slice(c * P, (c + 1) * P)
            nc.vector.tensor_tensor(out=eo_k_of[b][:, d, :],
                                    in0=eo_banks[(b, c)][:].rearrange("m t d -> m d t"),
                                    in1=b2_wide[:, d, :], op=ALU.add)

        def quantise_eo(b):
            nc.vector.quantize_mx(out=eo_codes[:, b, :].bitcast(FP8X4), scales=eo_scales[:, b, :],
                                  in_=eo_k_of[b][:].rearrange("m d t -> m (d t)"))

        acc_of, o_of = {}, {}

        def combine(g, tiles=range(J)):
            b = g // GROUPS_PER_BATCH
            for j in tiles:
                acc = psum_mm.tile([P, D], F32, tag="bank_mm")
                nc.tensor.matmul_mx(out=acc[:],
                                    lhsT=codes_of[g][:, j, :].bitcast(FP8X4),
                                    lhsT_scale=scales_of[g][:, j, :],
                                    rhs=eo_codes[:, b, :].bitcast(FP8X4),
                                    rhs_scale=eo_scales[:, b, :],
                                    start=True, stop=True)
                acc_of[(g, j)] = acc

        def take_out(g, j, copy):
            if j % 2 == 0:
                o = outs.tile([P, 2, D], F32)
                o_of[(g, j // 2)] = o
            copy(out=o_of[(g, j // 2)][:, j % 2, :], in_=acc_of[(g, j)][:])

        def store_tile(g, j):
            rows = out_rows[g * P * J:(g + 1) * P * J, :].rearrange("(p j) d -> p j d", j=J)
            nc.sync.dma_start(out=rows[:, j:j + 1, :], in_=o_of[(g, j // 2)][:, j % 2:j % 2 + 1, :])

        def store(g, half):
            rows = out_rows[g * P * J:(g + 1) * P * J, :].rearrange("(p j) d -> p j d", j=J)
            nc.sync.dma_start(out=rows[:, 2 * half:2 * half + 2, :], in_=o_of[(g, half)][:])

        h_by_tile = h.rearrange("b e s k -> (b e s) k").rearrange("(n p) k -> p n k", p=P)
        scale_rows = w2_scales.rearrange("g (qq r) n -> r qq g n", r=4)
        w2_words_by_p = w2_words.rearrange("g p n t -> p g (n t)").bitcast(I32)

        def load_h(first, last):
            nc.sync.dma_start(out=h_rows[:, T * first:T * last, :], in_=h_by_tile[:, T * first:T * last, :])

        def load_w2(t):
            nc.sync.dma_start(out=w2_codes[:, Q * t:Q * t + Q, :].bitcast(I32),
                              in_=w2_words_by_p[:, Q * t:Q * t + Q, :])

        load(0)
        nc.sync.dma_start(out=b2_rows[0:E, :], in_=b2)
        load(1)
        load_h(0, 2)
        load(2)
        load(3)
        for r in range(4):
            nc.sync.dma_start(out=w2_planes[r:P:32, :, :].bitcast(I32), in_=scale_rows[r].bitcast(I32))
        load_w2(0)
        load_w2(1)
        load(4)
        load_w2(2)
        load_w2(3)
        load(5)
        load_h(2, 4)

        TURN = {0: 0, 1: 1, 3: 2, 5: 3}
        SPREAD = {1: 0, 3: 1, 6: 2, 10: 3}
        MULTIPLY = {1: [(0, c, t) for t in (0,) for c in range(D_CHUNKS)],
                    2: [(0, c, t) for t in (1, 2, 3) for c in range(D_CHUNKS)],
                    3: [(1, 0, t) for t in range(T)], 4: [(1, c, t) for c in (1, 2) for t in range(T)], 5: [(1, 3, t) for t in range(T)]}
        for b in range(2, B):
            for c in range(D_CHUNKS):
                MULTIPLY.setdefault(4 * b - 2 + c - (b == 3 and c > 0), []).extend([(b, c, t) for t in range(T)])

        added = -1
        made = -1
        combined = 0
        pending = []
        for s in range(FIRST_STEP, GROUPS - 1):
            draining = s >= GROUPS
            load(s + LOAD_AHEAD)

            if added > made:
                quantise_eo(added)
                made = added
            if s == FIRST_STEP:
                for i in range(1):
                    tiles = slice(i * J // 1, (i + 1) * J // 1)
                    for level in range(FOLDS):
                        fold_max(0, level, tiles)
                    finish_max(0, tiles)
            else:
                fold_max(s + 2, 0)
                quantise(s - 2)
                fold_max(s + 2, 1)
            if s - 1 in TURN:
                quantise_h(TURN[s - 1])
            if s in SPREAD:
                spread(SPREAD[s])
            invert_sum(s)
            normalise(s, range((4 if s == 0 else 2), J), nc.gpsimd)
            transposes(s - 1)
            top = s - 2 if draining else s - LAG
            ready = [g for g in range(combined, GROUPS) if g <= top and g // GROUPS_PER_BATCH <= made][:2]
            combined += len(ready)
            for g in ready:
                combine(g)
            if s == -1 and [0, 1]:
                widen_b2([0, 1])
            exps(s + 1, range(0, (4 if s == 3 else 3)))
            if s == -1 and []:
                widen_b2([])
            if s == 0 and []:
                widen_b2([])
            copy_out(s - 1, 0, False)
            for b, c in pending:
                add_b2(b, c)
                if c == D_CHUNKS - 1:
                    added = b
            pending = []
            if s > FIRST_STEP:
                finish_max(s + 2)
            copy_out(s - 1, 1, len(ready) == 0)
            normalise(s, range(0, (4 if s == 0 else 2)), nc.vector)
            for i, g in enumerate(ready):
                for half in range(2):
                    for j in (2 * half, 2 * half + 1):
                        on_vector = s >= GROUPS - 1 and j % 2 == 1
                        take_out(g, j, nc.vector.tensor_copy if on_vector else nc.scalar.copy)
                        if g == GROUPS - 1 and False:
                            nc.sync.dma_start(out=out_rows[g * P * J:(g + 1) * P * J, :].rearrange("(p j) d -> p j d", j=J)[:, j:j + 1, :], in_=o_of[(g, half)][:, j % 2:j % 2 + 1, :])
                    if not (g == GROUPS - 1 and False):
                        store(g, half)
                    if i == 0 and half == 0:
                        exps(s + 1, range((4 if s == 3 else 3), 4))
            if not ready:
                exps(s + 1, range((4 if s == 3 else 3), 4))
            if s == -1 and []:
                widen_b2([])
            if s in TURN:
                turn_h(TURN[s])
            if s == 0 and [2, 3]:
                widen_b2([2, 3])
            for b, c, t in MULTIPLY.get(s, []):
                if t == 0:
                    open_eo(b, c)
                multiply_eo(b, c, t)
                if t == T - 1:
                    pending.append((b, c))
            if s == 2 and True:
                for b, c in pending:
                    add_b2(b, c)
                pending = []
                added = 0
        last = GROUPS - 1
        first = combined
        assert first == last - 3 and added == B - 1

        def results(g, tiles, copies):
            for j, copy in zip(tiles, copies):
                take_out(g, j, copy)
                if g == last:
                    store_tile(g, j)
                elif j % 2 == 1:
                    store(g, j // 2)

        if made < added:
            quantise_eo(added)
        on_scalar, on_vector = nc.scalar.copy, nc.vector.tensor_copy
        transposes(last - 1)
        combine(last - 3)
        quantise(last - 2)
        copy_out(last - 1, 0, False)
        copy_out(last - 1, 1, False)
        invert_sum(last)
        results(last - 3, range(J), [on_scalar] * J)
        combine(last - 2, range(0, 2))
        normalise(last, range(0, 2), nc.vector)
        transposes(last, range(0, 1))
        normalise(last, range(2, J), nc.vector)
        combine(last - 2, range(2, J))
        results(last - 2, range(J), [on_scalar] * J)
        transposes(last, range(1, 2))
        quantise(last - 1)
        copy_out(last, 0, False)
        copy_out(last, 1, False)
        combine(last - 1)
        quantise(last)
        results(last - 1, range(J), [on_scalar, on_scalar, on_scalar, on_vector])
        combine(last)
        results(last, range(J), [on_scalar, on_vector, on_scalar, on_vector])
